import numpy as np
import ml_dtypes


def mxq(x, axis, fmt="e4m3"):
    dtype, down = {"e4m3": (ml_dtypes.float8_e4m3fn, 7), "e5m2": (ml_dtypes.float8_e5m2, 14)}[fmt]
    v = np.moveaxis(np.asarray(x, np.float32).astype(ml_dtypes.bfloat16).astype(np.float64), axis, -1)
    blocks = v.reshape(v.shape[:-1] + (-1, 32))
    amax = np.abs(blocks).max(-1, keepdims=True)
    byte = np.maximum(np.where(amax > 0, np.frexp(amax)[1] - 1 + 127, 0) - down, 1)
    scale = np.exp2(byte - 127.0)
    codes = (blocks / scale).astype(np.float32).astype(dtype).astype(np.float64)
    return np.moveaxis((codes * scale).reshape(v.shape), -1, axis)


WIDE = False


def mx_kscale(k):
    if not WIDE:
        return np.ones(k)
    levels = np.array([10, -10, 5, -5, 0])
    a = np.random.permutation(np.resize(levels, k // 512 * 4)).reshape(k // 512, 4)
    idx = np.arange(k)
    return np.exp2(a[idx // 512, idx % 128 // 32])


BF16 = ml_dtypes.bfloat16


def bf(x):
    return np.asarray(x, np.float32).astype(BF16)


def f64(x):
    return np.asarray(x).astype(np.float64)


E2M1 = np.array([0.0, 0.5, 1.0, 1.5, 2.0, 3.0, 4.0, 6.0, -0.0, -0.5, -1.0, -1.5, -2.0, -3.0, -4.0, -6.0])


def pack_weight(w, fmt):
    k, n = w.shape
    w = f64(bf(w)).reshape(k // 32, 32, n)
    amax = np.abs(w).max(1)
    if fmt == "e4m3":
        byte = np.frexp(amax)[1] - 1 + 127 - 7
    else:
        mant, ex = np.frexp(amax / 6.0)
        byte = np.where(mant > 0.5, ex, ex - 1) + 127
    byte = np.clip(np.where(amax > 0, byte, 1), 1, 254)
    scaled = (w * np.exp2(127.0 - byte)[:, None, :]).reshape(k, n).astype(np.float32)
    by_word = np.ascontiguousarray(scaled.reshape(k // 512, 128, 4, n).transpose(0, 1, 3, 2))
    if fmt == "e4m3":
        words = by_word.astype(ml_dtypes.float8_e4m3fn).view(np.uint8)
    else:
        c = by_word.astype(ml_dtypes.float4_e2m1fn).view(np.uint8) & 0xF
        words = c[..., 0::2] | (c[..., 1::2] << 4)
    return np.ascontiguousarray(words), np.ascontiguousarray(byte.astype(np.uint8).reshape(k // 512, 16, n))


def unpack_weight(words, scales, fmt):
    g, p, n, _ = words.shape
    if fmt == "e4m3":
        vals = np.ascontiguousarray(words).view(ml_dtypes.float8_e4m3fn).astype(np.float64)
    else:
        nib = np.empty((g, p, n, 4), np.uint8)
        nib[..., 0::2] = words & 0xF
        nib[..., 1::2] = words >> 4
        vals = E2M1[nib]
    vals = vals * np.repeat(np.exp2(scales.astype(np.float64) - 127.0), 8, axis=1)[..., None]
    return vals.transpose(0, 1, 3, 2).reshape(g * 512, n)

def pack4(w):
    words, scales = pack_weight(w, "e2m1")
    return words.reshape(words.shape[0], 128, -1), scales


def unpack4(words, scales):
    return unpack_weight(words.reshape(words.shape[0], 128, -1, 2), scales, "e2m1")


B, S, H, D = 2, 2048, 8, 64
E = H * D
HALF = D // 2


def rotate_half(u):
    u1, u2 = np.split(u, 2, axis=-1)
    return np.concatenate([-u2, u1], axis=-1)


def apply_rope(t, sin, cos):
    x1, x2 = np.split(t, 2, axis=-1)
    x_rot = x1 * cos + rotate_half(x1) * sin
    return np.concatenate([x_rot, x2], axis=-1)


def setup_inputs():
    s = mx_kscale(E)
    th = np.random.uniform(0.0, 2.0 * np.pi, (S, HALF))
    x = bf(np.random.standard_normal((B, S, E)) * s)
    words, scales = pack4(np.random.standard_normal((E, 3 * E)) / np.sqrt(E) / s[:, None])
    return {"x": x,
            "W_qkv_words": words,
            "W_qkv_scales": scales,
            "b_qkv": bf(np.random.standard_normal(3 * E) * 0.2),
            "sin_tab": bf(np.sin(th)),
            "cos_tab": bf(np.cos(th))}


def reference(x, W_qkv_words, W_qkv_scales, b_qkv, sin_tab, cos_tab):
    qkv = (mxq(f64(x), 2, "e4m3") @ unpack4(W_qkv_words, W_qkv_scales)) + f64(b_qkv)
    q, k, v = np.split(qkv, 3, axis=-1)
    q = q.reshape(B, S, H, D)
    k = k.reshape(B, S, H, D)
    v = v.reshape(B, S, H, D)
    sin = f64(sin_tab)[None, :, None, :]
    cos = f64(cos_tab)[None, :, None, :]
    q_rot = apply_rope(q, sin, cos)
    k_rot = apply_rope(k, sin, cos)
    return q_rot, k_rot, v

@@ -1,0 +1,262 @@
+from contextlib import ExitStack
+
+import concourse.mybir as mybir
+from concourse.masks import make_identity
+
+F32 = mybir.dt.float32
+BF16 = mybir.dt.bfloat16
+I32 = mybir.dt.int32
+U32 = mybir.dt.uint32
+U8 = mybir.dt.uint8
+FP8X4 = mybir.dt.float8_e4m3fn_x4
+FP4X4 = mybir.dt.float4_e2m1fn_x4
+ALU = mybir.AluOpType
+IDENTITY = mybir.ActivationFunctionType.Identity
+
+P = 128
+PACK = 4
+BATCH, SEQ, HEADS, HEAD_DIM = 2, 2048, 8, 64
+E = HEADS * HEAD_DIM
+TURNED = HEAD_DIM // 2
+HALF = TURNED // 2
+QK_HEADS = 2 * HEADS
+TILES = 4
+GROUP = TILES * P
+GROUPS = BATCH * SEQ // GROUP
+SEQ_GROUPS = SEQ // GROUP
+BLOCKS = E // P
+
+FLOPS = 2 * BATCH * SEQ * E * 3 * E
+
+
+def tile_improvedattention_pa_t_kernel(
+    tc, x, W_qkv_words, W_qkv_scales, b_qkv, sin_tab, cos_tab, out_0, out_1, out_2
+):
+    nc = tc.nc
+
+    x_groups = x.rearrange("b (sg p t) k -> (b sg) p (t k)", sg=SEQ_GROUPS, p=P, t=TILES)
+    out_groups = [
+        out.rearrange("b (sg p t) h d -> (b sg) p (t h d)", sg=SEQ_GROUPS, p=P, t=TILES)
+        for out in (out_0, out_1, out_2)
+    ]
+
+    with ExitStack() as ctx:
+        const = ctx.enter_context(tc.tile_pool(name="const", bufs=1))
+        x_pool = ctx.enter_context(tc.tile_pool(name="x_pool", bufs=GROUPS))
+        stage = ctx.enter_context(tc.tile_pool(name="stage", bufs=2))
+        outs = ctx.enter_context(tc.tile_pool(name="outs", bufs=3))
+        psum_x = ctx.enter_context(tc.psum_pool(name="psum_x", bufs=2))
+        psum_feat = ctx.enter_context(tc.psum_pool(name="psum_feat", bufs=2))
+        psum_tok = ctx.enter_context(tc.psum_pool(name="psum_tok", bufs=2))
+        psum_back = ctx.enter_context(tc.psum_pool(name="psum_back", bufs=2))
+
+        x_tiles = []
+        for g in range(GROUPS):
+            x_sb = x_pool.tile([P, TILES * E], BF16)
+            x_tiles.append(x_sb)
+        nc.sync.dma_start(out=x_tiles[0][:], in_=x_groups[0])
+
+        w_raw = const.tile([P, 2 * 3 * E], U8, align_bytes=64)
+        nc.sync.dma_start(
+            out=w_raw[:].bitcast(I32),
+            in_=W_qkv_words.rearrange("o p n -> (o p) n").bitcast(I32),
+        )
+        ws_raw = const.tile([P, 3 * E], U8, align_bytes=64)
+        nc.vector.memset(ws_raw[:].bitcast(I32), 0)
+        scale_rows = W_qkv_scales.rearrange("o q n -> (o q) n")
+        for quadrant in range(4):
+            nc.sync.dma_start(
+                out=ws_raw[32 * quadrant : 32 * quadrant + 4, :].bitcast(I32),
+                in_=scale_rows[4 * quadrant : 4 * quadrant + 4, :].bitcast(I32),
+            )
+
+        bias_rows = const.tile([P, 3 * E], BF16)
+        nc.sync.dma_start(out=bias_rows[:], in_=b_qkv.partition_broadcast(P))
+
+        tables = const.tile([P, 2, SEQ_GROUPS * TILES, TURNED], BF16)
+        for which, table in enumerate((cos_tab, sin_tab)):
+            nc.sync.dma_start(
+                out=tables[:, which].rearrange("p (sg t) j -> p sg (t j)", sg=SEQ_GROUPS),
+                in_=table.rearrange("(sg p t) j -> p sg (t j)", sg=SEQ_GROUPS, p=P, t=TILES),
+            )
+        for g in range(1, GROUPS):
+            nc.sync.dma_start(out=x_tiles[g][:], in_=x_groups[g])
+
+        ident = const.tile([P, P], F32)
+        make_identity(nc, ident[:])
+
+        w_qk = const.tile([P, 2 * 2 * E], U8, align_bytes=64)
+        nc.vector.tensor_copy(
+            out=w_qk[:].bitcast(I32).rearrange("p (c h b) -> p c h b", c=2, h=QK_HEADS),
+            in_=w_raw[:, 0 : 2 * 2 * E].bitcast(I32).rearrange("p (h c b) -> p c h b", h=QK_HEADS, c=2),
+        )
+        ws_qk = const.tile([P, 2 * E], U8, align_bytes=64)
+        nc.vector.tensor_copy(
+            out=ws_qk[:].bitcast(I32).rearrange("p (c h b) -> p c h b", c=2, h=QK_HEADS),
+            in_=ws_raw[:, 0 : 2 * E].bitcast(I32).rearrange("p (h c b) -> p c h b", h=QK_HEADS, c=2),
+        )
+
+        def weight_columns(kind, first, count):
+            words, plane, base = {
+                "turned": (w_qk, ws_qk, 0),
+                "plain": (w_qk, ws_qk, E),
+                "v": (w_raw, ws_raw, 2 * E),
+            }[kind]
+            lo = base + first
+            return words[:, 2 * lo : 2 * (lo + count)].bitcast(FP4X4), plane[:, lo : lo + count]
+
+        diagonal = const.tile([P, 2 * BLOCKS, P], F32)
+        nc.vector.tensor_tensor(
+            out=diagonal[:, 0:BLOCKS, :].rearrange("p k (h j) -> p k h j", j=TURNED),
+            in0=bias_rows[:, 0 : 2 * E].rearrange(
+                "p (k h c j) -> p k h c j", k=BLOCKS, c=2, j=TURNED
+            )[:, :, :, 0, :],
+            in1=ident[:]
+            .rearrange("p (h j) -> p h j", j=TURNED)
+            .unsqueeze(1)
+            .to_broadcast([P, BLOCKS, P // TURNED, TURNED]),
+            op=ALU.mult,
+        )
+        nc.vector.tensor_tensor(
+            out=diagonal[:, BLOCKS : 2 * BLOCKS, :],
+            in0=bias_rows[:, 2 * E : 3 * E].rearrange("p (k c) -> p k c", k=BLOCKS),
+            in1=ident[:].unsqueeze(1).to_broadcast([P, BLOCKS, P]),
+            op=ALU.mult,
+        )
+        bias_col = const.tile([P, 2 * BLOCKS], F32)
+        nc.vector.tensor_reduce(
+            out=bias_col[:], in_=diagonal[:], axis=mybir.AxisListType.X, op=ALU.add
+        )
+        plain_bias = bias_rows[:, 0 : 2 * E].rearrange(
+            "p (q h c j) -> p q h c j", q=2, h=HEADS, c=2
+        )[:, :, :, 1, :]
+
+        factors = const.tile([P, SEQ_GROUPS * TILES, 2, TURNED], BF16)
+        nc.vector.tensor_copy(out=factors[:, :, 0, :], in_=tables[:, 0])
+        nc.vector.tensor_copy(out=factors[:, :, 1, 0:HALF], in_=tables[:, 1, :, HALF:TURNED])
+        nc.vector.tensor_copy(out=factors[:, :, 1, HALF:TURNED], in_=tables[:, 1, :, 0:HALF])
+
+        def quantise_group(g):
+            x_words = x_tiles[g][:].bitcast(F32)
+            grouped = stage.tile([P, GROUP * PACK], BF16, align_bytes=64)
+            grouped_words = grouped[:].bitcast(F32).rearrange("p (c u) -> p c u", u=2)
+            for pair in range(TILES // 2):
+                xt = psum_x.tile([P, 2, 2, P], F32)
+                for i in range(2):
+                    first = (2 * pair + i) * (E // 2)
+                    for u in range(2):
+                        nc.tensor.transpose(
+                            out=xt[:, i, u, :],
+                            in_=x_words[:, first + u : first + E // 2 : 2],
+                            identity=ident[:],
+                        )
+                nc.scalar.copy(
+                    out=grouped_words[:, 2 * P * pair : 2 * P * (pair + 1), :].rearrange(
+                        "p (i c) u -> p i c u", i=2
+                    ),
+                    in_=xt[:].rearrange("p i u c -> p i c u"),
+                )
+            codes = stage.tile([P, GROUP], U32, align_bytes=64)
+            scales = stage.tile([P, GROUP], U8, align_bytes=64)
+            nc.vector.quantize_mx(out=codes[:].bitcast(FP8X4), scales=scales[:], in_=grouped[:])
+            return codes, scales
+
+        def feature_major(codes, scales, feat):
+            for k in range(2 * BLOCKS):
+                kind = "turned" if k < BLOCKS else "v"
+                w_words, w_plane = weight_columns(kind, (k % BLOCKS) * P, P)
+                acc = psum_feat.tile([P, GROUP], F32)
+                nc.tensor.matmul_mx(
+                    out=acc[:],
+                    lhsT=w_words,
+                    lhsT_scale=w_plane,
+                    rhs=codes[:].bitcast(FP8X4),
+                    rhs_scale=scales[:],
+                    start=True,
+                    stop=True,
+                )
+                nc.scalar.activation(
+                    out=feat[:, k, :], in_=acc[:], func=IDENTITY, bias=bias_col[:, k : k + 1], scale=1.0
+                )
+
+        def plain_features(codes, scales, qk_out):
+            w_words, w_plane = weight_columns("plain", 0, E)
+            for t in range(TILES):
+                acc = psum_tok.tile([P, E], F32)
+                nc.tensor.matmul_mx(
+                    out=acc[:],
+                    lhsT=codes[:, t * P : (t + 1) * P].bitcast(FP8X4),
+                    lhsT_scale=scales[:, t * P : (t + 1) * P],
+                    rhs=w_words,
+                    rhs_scale=w_plane,
+                    start=True,
+                    stop=True,
+                )
+                nc.vector.tensor_tensor(
+                    out=qk_out[:, :, t, :, TURNED:HEAD_DIM],
+                    in0=acc[:].rearrange("p (q h j) -> p q h j", q=2, h=HEADS),
+                    in1=plain_bias,
+                    op=ALU.add,
+                )
+
+        def back_to_tokens(feat, first_block, t):
+            back = psum_back.tile([P, E], F32)
+            for k in range(BLOCKS):
+                nc.tensor.transpose(
+                    out=back[:, k * P : (k + 1) * P],
+                    in_=feat[:, first_block + k, t * P : (t + 1) * P],
+                    identity=ident[:],
+                )
+            return back
+
+        def turned_features(g, feat, qk_out):
+            products = stage.tile([P, TILES, 2, E], F32)
+            for t in range(TILES):
+                u = back_to_tokens(feat, 0, t)
+                shape = [P, 2, QK_HEADS, TURNED]
+                nc.vector.tensor_tensor(
+                    out=products[:, t].rearrange("p f (h j) -> p f h j", h=QK_HEADS),
+                    in0=u[:].rearrange("p (h j) -> p h j", h=QK_HEADS).unsqueeze(1).to_broadcast(shape),
+                    in1=factors[:, (g % SEQ_GROUPS) * TILES + t].unsqueeze(2).to_broadcast(shape),
+                    op=ALU.mult,
+                )
+            split = products[:].rearrange(
+                "p t f (q h a i) -> p t f q h a i", q=2, h=HEADS, a=2
+            )
+            for q in range(2):
+                nc.gpsimd.tensor_tensor(
+                    out=qk_out[:, q, :, :, 0:HALF],
+                    in0=split[:, :, 0, q, :, 0, :],
+                    in1=split[:, :, 1, q, :, 1, :],
+                    op=ALU.subtract,
+                )
+                nc.gpsimd.tensor_tensor(
+                    out=qk_out[:, q, :, :, HALF:TURNED],
+                    in0=split[:, :, 0, q, :, 1, :],
+                    in1=split[:, :, 1, q, :, 0, :],
+                    op=ALU.add,
+                )
+
+        def v_features(feat, v_out):
+            for t in range(TILES):
+                back = back_to_tokens(feat, BLOCKS, t)
+                nc.scalar.copy(out=v_out[:, t, :], in_=back[:])
+
+        quantised = quantise_group(0)
+        for g in range(GROUPS):
+            codes, scales = quantised
+            feat = stage.tile([P, 2 * BLOCKS, GROUP], F32)
+            qk_out = outs.tile([P, 2, TILES, HEADS, HEAD_DIM], F32)
+            v_out = outs.tile([P, TILES, E], F32)
+
+            feature_major(codes, scales, feat)
+            if g + 1 < GROUPS:
+                quantised = quantise_group(g + 1)
+            plain_features(codes, scales, qk_out)
+            turned_features(g, feat, qk_out)
+            for q in range(2):
+                nc.sync.dma_start(
+                    out=out_groups[q][g], in_=qk_out[:, q].rearrange("p t h d -> p (t h d)")
+                )
+            v_features(feat, v_out)
+            nc.sync.dma_start(out=out_groups[2][g], in_=v_out[:].rearrange("p t n -> p (t n)"))

@@ -41,25 +41,43 @@ def tile_improvedattention_pa_t_kernel(
     ]
 
     with ExitStack() as ctx:
+        ctx.enter_context(tc.manual_schedule())
         const = ctx.enter_context(tc.tile_pool(name="const", bufs=1))
         x_pool = ctx.enter_context(tc.tile_pool(name="x_pool", bufs=GROUPS))
         stage = ctx.enter_context(tc.tile_pool(name="stage", bufs=2))
         outs = ctx.enter_context(tc.tile_pool(name="outs", bufs=3))
-        psum_x = ctx.enter_context(tc.psum_pool(name="psum_x", bufs=2))
+        psum_x = ctx.enter_context(tc.psum_pool(name="psum_x", bufs=1))
         psum_feat = ctx.enter_context(tc.psum_pool(name="psum_feat", bufs=2))
-        psum_tok = ctx.enter_context(tc.psum_pool(name="psum_tok", bufs=2))
-        psum_back = ctx.enter_context(tc.psum_pool(name="psum_back", bufs=2))
+        psum_plain = ctx.enter_context(tc.psum_pool(name="psum_plain", bufs=1))
+        psum_turned = ctx.enter_context(tc.psum_pool(name="psum_turned", bufs=2))
+        psum_v = ctx.enter_context(tc.psum_pool(name="psum_v", bufs=2))
 
         x_tiles = []
         for g in range(GROUPS):
             x_sb = x_pool.tile([P, TILES * E], BF16)
             x_tiles.append(x_sb)
-        nc.sync.dma_start(out=x_tiles[0][:], in_=x_groups[0])
+
+        def load_x(g):
+            for pair in range(TILES // 2):
+                cols = slice(2 * E * pair, 2 * E * (pair + 1))
+                nc.sync.dma_start(out=x_tiles[g][:, cols], in_=x_groups[g][:, cols])
+
+        load_x(0)
 
         w_raw = const.tile([P, 2 * 3 * E], U8, align_bytes=64)
         nc.sync.dma_start(
             out=w_raw[:].bitcast(I32),
             in_=W_qkv_words.rearrange("o p n -> (o p) n").bitcast(I32),
+        )
+        bias_blocks = const.tile([P, P], BF16)
+        nc.vector.memset(bias_blocks[:], 0.0)
+        nc.sync.dma_start(
+            out=bias_blocks[0:BLOCKS, :].rearrange("k (h j) -> k h j", j=TURNED),
+            in_=b_qkv[0 : 2 * E].rearrange("(k h c j) -> k h c j", k=BLOCKS, c=2, j=TURNED)[:, :, 0, :],
+        )
+        nc.sync.dma_start(
+            out=bias_blocks[BLOCKS : 2 * BLOCKS, :],
+            in_=b_qkv[2 * E : 3 * E].rearrange("(k c) -> k c", k=BLOCKS),
         )
         ws_raw = const.tile([P, 3 * E], U8, align_bytes=64)
         nc.vector.memset(ws_raw[:].bitcast(I32), 0)
@@ -69,21 +87,28 @@ def tile_improvedattention_pa_t_kernel(
                 out=ws_raw[32 * quadrant : 32 * quadrant + 4, :].bitcast(I32),
                 in_=scale_rows[4 * quadrant : 4 * quadrant + 4, :].bitcast(I32),
             )
-
-        bias_rows = const.tile([P, 3 * E], BF16)
-        nc.sync.dma_start(out=bias_rows[:], in_=b_qkv.partition_broadcast(P))
-
+        qk_bias_rows = const.tile([P, 2 * E], BF16)
+        nc.sync.dma_start(out=qk_bias_rows[:], in_=b_qkv[0 : 2 * E].partition_broadcast(P))
+        load_x(1)
         tables = const.tile([P, 2, SEQ_GROUPS * TILES, TURNED], BF16)
         for which, table in enumerate((cos_tab, sin_tab)):
             nc.sync.dma_start(
                 out=tables[:, which].rearrange("p (sg t) j -> p sg (t j)", sg=SEQ_GROUPS),
                 in_=table.rearrange("(sg p t) j -> p sg (t j)", sg=SEQ_GROUPS, p=P, t=TILES),
             )
-        for g in range(1, GROUPS):
-            nc.sync.dma_start(out=x_tiles[g][:], in_=x_groups[g])
+        for g in range(2, GROUPS):
+            load_x(g)
 
         ident = const.tile([P, P], F32)
         make_identity(nc, ident[:])
+
+        factors = const.tile([P, SEQ_GROUPS * TILES, 2, TURNED], BF16)
+        nc.gpsimd.tensor_copy(out=factors[:, :, 0, :], in_=tables[:, 0])
+        nc.gpsimd.tensor_copy(out=factors[:, :, 1, 0:HALF], in_=tables[:, 1, :, HALF:TURNED])
+        nc.gpsimd.tensor_copy(out=factors[:, :, 1, HALF:TURNED], in_=tables[:, 1, :, 0:HALF])
+
+        bias_blocks_f32 = const.tile([P, P], F32)
+        nc.vector.tensor_copy(out=bias_blocks_f32[:], in_=bias_blocks[:])
 
         w_qk = const.tile([P, 2 * 2 * E], U8, align_bytes=64)
         nc.vector.tensor_copy(
@@ -105,158 +130,151 @@ def tile_improvedattention_pa_t_kernel(
             lo = base + first
             return words[:, 2 * lo : 2 * (lo + count)].bitcast(FP4X4), plane[:, lo : lo + count]
 
-        diagonal = const.tile([P, 2 * BLOCKS, P], F32)
-        nc.vector.tensor_tensor(
-            out=diagonal[:, 0:BLOCKS, :].rearrange("p k (h j) -> p k h j", j=TURNED),
-            in0=bias_rows[:, 0 : 2 * E].rearrange(
-                "p (k h c j) -> p k h c j", k=BLOCKS, c=2, j=TURNED
-            )[:, :, :, 0, :],
-            in1=ident[:]
-            .rearrange("p (h j) -> p h j", j=TURNED)
-            .unsqueeze(1)
-            .to_broadcast([P, BLOCKS, P // TURNED, TURNED]),
-            op=ALU.mult,
-        )
-        nc.vector.tensor_tensor(
-            out=diagonal[:, BLOCKS : 2 * BLOCKS, :],
-            in0=bias_rows[:, 2 * E : 3 * E].rearrange("p (k c) -> p k c", k=BLOCKS),
-            in1=ident[:].unsqueeze(1).to_broadcast([P, BLOCKS, P]),
-            op=ALU.mult,
-        )
-        bias_col = const.tile([P, 2 * BLOCKS], F32)
-        nc.vector.tensor_reduce(
-            out=bias_col[:], in_=diagonal[:], axis=mybir.AxisListType.X, op=ALU.add
-        )
-        plain_bias = bias_rows[:, 0 : 2 * E].rearrange(
-            "p (q h c j) -> p q h c j", q=2, h=HEADS, c=2
-        )[:, :, :, 1, :]
+        plain_bias = qk_bias_rows[:].rearrange("p (q h c j) -> p q h c j", q=2, h=HEADS, c=2)[
+            :, :, :, 1, :
+        ]
 
-        factors = const.tile([P, SEQ_GROUPS * TILES, 2, TURNED], BF16)
-        nc.vector.tensor_copy(out=factors[:, :, 0, :], in_=tables[:, 0])
-        nc.vector.tensor_copy(out=factors[:, :, 1, 0:HALF], in_=tables[:, 1, :, HALF:TURNED])
-        nc.vector.tensor_copy(out=factors[:, :, 1, HALF:TURNED], in_=tables[:, 1, :, 0:HALF])
-
-        def quantise_group(g):
+        def transpose_x(g, pair, grouped):
             x_words = x_tiles[g][:].bitcast(F32)
-            grouped = stage.tile([P, GROUP * PACK], BF16, align_bytes=64)
+            xt = psum_x.tile([P, 2, 2, P], F32)
+            for i in range(2):
+                first = (2 * pair + i) * (E // 2)
+                for u in range(2):
+                    nc.tensor.transpose(
+                        out=xt[:, i, u, :],
+                        in_=x_words[:, first + u : first + E // 2 : 2],
+                        identity=ident[:],
+                    )
             grouped_words = grouped[:].bitcast(F32).rearrange("p (c u) -> p c u", u=2)
-            for pair in range(TILES // 2):
-                xt = psum_x.tile([P, 2, 2, P], F32)
-                for i in range(2):
-                    first = (2 * pair + i) * (E // 2)
-                    for u in range(2):
-                        nc.tensor.transpose(
-                            out=xt[:, i, u, :],
-                            in_=x_words[:, first + u : first + E // 2 : 2],
-                            identity=ident[:],
-                        )
-                nc.scalar.copy(
-                    out=grouped_words[:, 2 * P * pair : 2 * P * (pair + 1), :].rearrange(
-                        "p (i c) u -> p i c u", i=2
-                    ),
-                    in_=xt[:].rearrange("p i u c -> p i c u"),
-                )
+            nc.scalar.copy(
+                out=grouped_words[:, 2 * P * pair : 2 * P * (pair + 1), :].rearrange(
+                    "p (i c) u -> p i c u", i=2
+                ),
+                in_=xt[:].rearrange("p i u c -> p i c u"),
+            )
+
+        def quantise(grouped):
             codes = stage.tile([P, GROUP], U32, align_bytes=64)
             scales = stage.tile([P, GROUP], U8, align_bytes=64)
             nc.vector.quantize_mx(out=codes[:].bitcast(FP8X4), scales=scales[:], in_=grouped[:])
             return codes, scales
 
-        def feature_major(codes, scales, feat):
-            for k in range(2 * BLOCKS):
-                kind = "turned" if k < BLOCKS else "v"
-                w_words, w_plane = weight_columns(kind, (k % BLOCKS) * P, P)
-                acc = psum_feat.tile([P, GROUP], F32)
-                nc.tensor.matmul_mx(
-                    out=acc[:],
-                    lhsT=w_words,
-                    lhsT_scale=w_plane,
-                    rhs=codes[:].bitcast(FP8X4),
-                    rhs_scale=scales[:],
-                    start=True,
-                    stop=True,
-                )
-                nc.scalar.activation(
-                    out=feat[:, k, :], in_=acc[:], func=IDENTITY, bias=bias_col[:, k : k + 1], scale=1.0
-                )
+        def feature_major(codes, scales, feat, k):
+            kind = "turned" if k < BLOCKS else "v"
+            w_words, w_plane = weight_columns(kind, (k % BLOCKS) * P, P)
+            acc = psum_feat.tile([P, GROUP], F32)
+            nc.tensor.matmul_mx(
+                out=acc[:],
+                lhsT=w_words,
+                lhsT_scale=w_plane,
+                rhs=codes[:].bitcast(FP8X4),
+                rhs_scale=scales[:],
+                start=True,
+                stop=True,
+            )
+            nc.scalar.activation(
+                out=feat[:, k, :], in_=acc[:], func=IDENTITY, bias=bias_col[:, k : k + 1], scale=1.0
+            )
 
-        def plain_features(codes, scales, qk_out):
+        def plain_features(codes, scales, qk_out, t):
             w_words, w_plane = weight_columns("plain", 0, E)
-            for t in range(TILES):
-                acc = psum_tok.tile([P, E], F32)
-                nc.tensor.matmul_mx(
-                    out=acc[:],
-                    lhsT=codes[:, t * P : (t + 1) * P].bitcast(FP8X4),
-                    lhsT_scale=scales[:, t * P : (t + 1) * P],
-                    rhs=w_words,
-                    rhs_scale=w_plane,
-                    start=True,
-                    stop=True,
-                )
-                nc.vector.tensor_tensor(
-                    out=qk_out[:, :, t, :, TURNED:HEAD_DIM],
-                    in0=acc[:].rearrange("p (q h j) -> p q h j", q=2, h=HEADS),
-                    in1=plain_bias,
-                    op=ALU.add,
-                )
+            plain = psum_plain.tile([P, E], F32)
+            nc.tensor.matmul_mx(
+                out=plain[:],
+                lhsT=codes[:, t * P : (t + 1) * P].bitcast(FP8X4),
+                lhsT_scale=scales[:, t * P : (t + 1) * P],
+                rhs=w_words,
+                rhs_scale=w_plane,
+                start=True,
+                stop=True,
+            )
+            nc.vector.tensor_tensor(
+                out=qk_out[:, :, t, :, TURNED:HEAD_DIM],
+                in0=plain[:].rearrange("p (q h j) -> p q h j", q=2, h=HEADS),
+                in1=plain_bias,
+                op=ALU.add,
+            )
 
-        def back_to_tokens(feat, first_block, t):
-            back = psum_back.tile([P, E], F32)
+        def back_to_tokens(bank, feat, first_block, t):
             for k in range(BLOCKS):
                 nc.tensor.transpose(
-                    out=back[:, k * P : (k + 1) * P],
+                    out=bank[:, k * P : (k + 1) * P],
                     in_=feat[:, first_block + k, t * P : (t + 1) * P],
                     identity=ident[:],
                 )
-            return back
 
-        def turned_features(g, feat, qk_out):
-            products = stage.tile([P, TILES, 2, E], F32)
-            for t in range(TILES):
-                u = back_to_tokens(feat, 0, t)
-                shape = [P, 2, QK_HEADS, TURNED]
-                nc.vector.tensor_tensor(
-                    out=products[:, t].rearrange("p f (h j) -> p f h j", h=QK_HEADS),
-                    in0=u[:].rearrange("p (h j) -> p h j", h=QK_HEADS).unsqueeze(1).to_broadcast(shape),
-                    in1=factors[:, (g % SEQ_GROUPS) * TILES + t].unsqueeze(2).to_broadcast(shape),
-                    op=ALU.mult,
-                )
-            split = products[:].rearrange(
-                "p t f (q h a i) -> p t f q h a i", q=2, h=HEADS, a=2
+        def turned_and_v_features(g, feat, qk_out, v_out, t):
+            u = psum_turned.tile([P, E], F32)
+            back_to_tokens(u, feat, 0, t)
+            v = psum_v.tile([P, E], F32)
+            back_to_tokens(v, feat, BLOCKS, t)
+            nc.scalar.copy(out=v_out[:, t, :], in_=v[:])
+
+            products = outs.tile([P, 2, E], F32)
+            shape = [P, 2, QK_HEADS, TURNED]
+            nc.vector.tensor_tensor(
+                out=products[:].rearrange("p f (h j) -> p f h j", h=QK_HEADS),
+                in0=u[:].rearrange("p (h j) -> p h j", h=QK_HEADS).unsqueeze(1).to_broadcast(shape),
+                in1=factors[:, (g % SEQ_GROUPS) * TILES + t].unsqueeze(2).to_broadcast(shape),
+                op=ALU.mult,
+            )
+            split = products[:].rearrange("p f (q h a i) -> p f q h a i", q=2, h=HEADS, a=2)
+            nc.gpsimd.tensor_tensor(
+                out=qk_out[:, :, t, :, 0:HALF],
+                in0=split[:, 0, :, :, 0, :],
+                in1=split[:, 1, :, :, 1, :],
+                op=ALU.subtract,
+            )
+            nc.gpsimd.tensor_tensor(
+                out=qk_out[:, :, t, :, HALF:TURNED],
+                in0=split[:, 0, :, :, 1, :],
+                in1=split[:, 1, :, :, 0, :],
+                op=ALU.add,
+            )
+
+        def store_pair(g, pair, qk_out, v_out):
+            tiles = slice(2 * pair, 2 * pair + 2)
+            cols = slice(2 * E * pair, 2 * E * (pair + 1))
+            nc.sync.dma_start(
+                out=out_groups[2][g][:, cols], in_=v_out[:, tiles, :].rearrange("p t n -> p (t n)")
             )
             for q in range(2):
-                nc.gpsimd.tensor_tensor(
-                    out=qk_out[:, q, :, :, 0:HALF],
-                    in0=split[:, :, 0, q, :, 0, :],
-                    in1=split[:, :, 1, q, :, 1, :],
-                    op=ALU.subtract,
-                )
-                nc.gpsimd.tensor_tensor(
-                    out=qk_out[:, q, :, :, HALF:TURNED],
-                    in0=split[:, :, 0, q, :, 1, :],
-                    in1=split[:, :, 1, q, :, 0, :],
-                    op=ALU.add,
-                )
-
-        def v_features(feat, v_out):
-            for t in range(TILES):
-                back = back_to_tokens(feat, BLOCKS, t)
-                nc.scalar.copy(out=v_out[:, t, :], in_=back[:])
-
-        quantised = quantise_group(0)
-        for g in range(GROUPS):
-            codes, scales = quantised
-            feat = stage.tile([P, 2 * BLOCKS, GROUP], F32)
-            qk_out = outs.tile([P, 2, TILES, HEADS, HEAD_DIM], F32)
-            v_out = outs.tile([P, TILES, E], F32)
-
-            feature_major(codes, scales, feat)
-            if g + 1 < GROUPS:
-                quantised = quantise_group(g + 1)
-            plain_features(codes, scales, qk_out)
-            turned_features(g, feat, qk_out)
-            for q in range(2):
                 nc.sync.dma_start(
-                    out=out_groups[q][g], in_=qk_out[:, q].rearrange("p t h d -> p (t h d)")
+                    out=out_groups[q][g][:, cols],
+                    in_=qk_out[:, q, tiles].rearrange("p t h d -> p (t h d)"),
                 )
-            v_features(feat, v_out)
-            nc.sync.dma_start(out=out_groups[2][g], in_=v_out[:].rearrange("p t n -> p (t n)"))
+
+        grouped = stage.tile([P, GROUP * PACK], BF16, align_bytes=64)
+        for pair in range(TILES // 2):
+            transpose_x(0, pair, grouped)
+        quantised = quantise(grouped)
+
+        bias_t = psum_turned.tile([P, P], F32, tag="u")
+        nc.tensor.transpose(out=bias_t[:], in_=bias_blocks_f32[:], identity=ident[:])
+        bias_col = const.tile([P, 2 * BLOCKS], F32)
+        nc.vector.tensor_copy(out=bias_col[:], in_=bias_t[:, 0 : 2 * BLOCKS])
+
+        held = {}
+        for i in range(GROUPS + 1):
+            if i < GROUPS:
+                codes, scales = quantised
+                feat = stage.tile([P, 2 * BLOCKS, GROUP], F32)
+                qk_out = outs.tile([P, 2, TILES, HEADS, HEAD_DIM], F32)
+                held[i] = (feat, qk_out)
+            if i >= 1:
+                v_out = outs.tile([P, TILES, E], F32)
+            if i + 1 < GROUPS:
+                grouped = stage.tile([P, GROUP * PACK], BF16, align_bytes=64)
+            for step in range(TILES):
+                if i < GROUPS:
+                    feature_major(codes, scales, held[i][0], step)
+                    feature_major(codes, scales, held[i][0], BLOCKS + step)
+                    plain_features(codes, scales, held[i][1], step)
+                if i >= 1:
+                    turned_and_v_features(i - 1, held[i - 1][0], held[i - 1][1], v_out, step)
+                if i + 1 < GROUPS and step < TILES // 2:
+                    transpose_x(i + 1, step, grouped)
+                if i + 1 < GROUPS and step == TILES // 2:
+                    quantised = quantise(grouped)
+                if i >= 1 and step % 2 == 1:
+                    store_pair(i - 1, step // 2, held[i - 1][1], v_out)

@@ -21,6 +21,7 @@ TURNED = HEAD_DIM // 2
 HALF = TURNED // 2
 QK_HEADS = 2 * HEADS
 TILES = 4
+PAIRS = TILES // 2
 GROUP = TILES * P
 GROUPS = BATCH * SEQ // GROUP
 SEQ_GROUPS = SEQ // GROUP
@@ -35,10 +36,13 @@ def tile_improvedattention_pa_t_kernel(
     nc = tc.nc
 
     x_groups = x.rearrange("b (sg p t) k -> (b sg) p (t k)", sg=SEQ_GROUPS, p=P, t=TILES)
-    out_groups = [
+    q_groups, k_groups, v_groups = [
         out.rearrange("b (sg p t) h d -> (b sg) p (t h d)", sg=SEQ_GROUPS, p=P, t=TILES)
         for out in (out_0, out_1, out_2)
     ]
+
+    def pair_columns(pair):
+        return slice(2 * E * pair, 2 * E * (pair + 1))
 
     with ExitStack() as ctx:
         ctx.enter_context(tc.manual_schedule())
@@ -58,8 +62,8 @@ def tile_improvedattention_pa_t_kernel(
             x_tiles.append(x_sb)
 
         def load_x(g):
-            for pair in range(TILES // 2):
-                cols = slice(2 * E * pair, 2 * E * (pair + 1))
+            for pair in range(PAIRS):
+                cols = pair_columns(pair)
                 nc.sync.dma_start(out=x_tiles[g][:, cols], in_=x_groups[g][:, cols])
 
         load_x(0)
@@ -87,8 +91,8 @@ def tile_improvedattention_pa_t_kernel(
                 out=ws_raw[32 * quadrant : 32 * quadrant + 4, :].bitcast(I32),
                 in_=scale_rows[4 * quadrant : 4 * quadrant + 4, :].bitcast(I32),
             )
-        qk_bias_rows = const.tile([P, 2 * E], BF16)
-        nc.sync.dma_start(out=qk_bias_rows[:], in_=b_qkv[0 : 2 * E].partition_broadcast(P))
+        bias_rows = const.tile([P, 3 * E], BF16)
+        nc.sync.dma_start(out=bias_rows[:], in_=b_qkv.partition_broadcast(P))
         load_x(1)
         tables = const.tile([P, 2, SEQ_GROUPS * TILES, TURNED], BF16)
         for which, table in enumerate((cos_tab, sin_tab)):
@@ -130,9 +134,8 @@ def tile_improvedattention_pa_t_kernel(
             lo = base + first
             return words[:, 2 * lo : 2 * (lo + count)].bitcast(FP4X4), plane[:, lo : lo + count]
 
-        plain_bias = qk_bias_rows[:].rearrange("p (q h c j) -> p q h c j", q=2, h=HEADS, c=2)[
-            :, :, :, 1, :
-        ]
+        plain_bias = bias_rows[:, 0 : 2 * E].rearrange("p (h c j) -> p h c j", h=QK_HEADS, c=2)[:, :, 1, :]
+        v_bias = bias_rows[:, 2 * E : 3 * E]
 
         def transpose_x(g, pair, grouped):
             x_words = x_tiles[g][:].bitcast(F32)
@@ -159,28 +162,34 @@ def tile_improvedattention_pa_t_kernel(
             nc.vector.quantize_mx(out=codes[:].bitcast(FP8X4), scales=scales[:], in_=grouped[:])
             return codes, scales
 
-        def feature_major(codes, scales, feat, k):
-            kind = "turned" if k < BLOCKS else "v"
-            w_words, w_plane = weight_columns(kind, (k % BLOCKS) * P, P)
+        def feature_major(xq, kind, k, feat):
+            codes, scales = xq
+            tokens = feat.shape[2]
+            w_words, w_plane = weight_columns(kind, k * P, P)
+            column = k if kind == "turned" else BLOCKS + k
             acc = psum_feat.tile([P, GROUP], F32)
             nc.tensor.matmul_mx(
-                out=acc[:],
+                out=acc[:, 0:tokens],
                 lhsT=w_words,
                 lhsT_scale=w_plane,
-                rhs=codes[:].bitcast(FP8X4),
-                rhs_scale=scales[:],
+                rhs=codes[:, 0:tokens].bitcast(FP8X4),
+                rhs_scale=scales[:, 0:tokens],
                 start=True,
                 stop=True,
             )
             nc.scalar.activation(
-                out=feat[:, k, :], in_=acc[:], func=IDENTITY, bias=bias_col[:, k : k + 1], scale=1.0
+                out=feat[:, k, :],
+                in_=acc[:, 0:tokens],
+                func=IDENTITY,
+                bias=bias_col[:, column : column + 1],
+                scale=1.0,
             )
 
-        def plain_features(codes, scales, qk_out, t):
-            w_words, w_plane = weight_columns("plain", 0, E)
-            plain = psum_plain.tile([P, E], F32)
+        def token_major(xq, kind, t, bank):
+            codes, scales = xq
+            w_words, w_plane = weight_columns(kind, 0, E)
             nc.tensor.matmul_mx(
-                out=plain[:],
+                out=bank[:],
                 lhsT=codes[:, t * P : (t + 1) * P].bitcast(FP8X4),
                 lhsT_scale=scales[:, t * P : (t + 1) * P],
                 rhs=w_words,
@@ -188,93 +197,118 @@ def tile_improvedattention_pa_t_kernel(
                 start=True,
                 stop=True,
             )
-            nc.vector.tensor_tensor(
-                out=qk_out[:, :, t, :, TURNED:HEAD_DIM],
-                in0=plain[:].rearrange("p (q h j) -> p q h j", q=2, h=HEADS),
-                in1=plain_bias,
-                op=ALU.add,
-            )
 
-        def back_to_tokens(bank, feat, first_block, t):
+        def back_to_tokens(feat, t, bank):
             for k in range(BLOCKS):
                 nc.tensor.transpose(
                     out=bank[:, k * P : (k + 1) * P],
-                    in_=feat[:, first_block + k, t * P : (t + 1) * P],
+                    in_=feat[:, k, t * P : (t + 1) * P],
                     identity=ident[:],
                 )
 
-        def turned_and_v_features(g, feat, qk_out, v_out, t):
-            u = psum_turned.tile([P, E], F32)
-            back_to_tokens(u, feat, 0, t)
-            v = psum_v.tile([P, E], F32)
-            back_to_tokens(v, feat, BLOCKS, t)
-            nc.scalar.copy(out=v_out[:, t, :], in_=v[:])
-
-            products = outs.tile([P, 2, E], F32)
+        def multiply_by_cos_and_sin(g, t, u, products):
             shape = [P, 2, QK_HEADS, TURNED]
             nc.vector.tensor_tensor(
-                out=products[:].rearrange("p f (h j) -> p f h j", h=QK_HEADS),
+                out=products[:, t % 2],
                 in0=u[:].rearrange("p (h j) -> p h j", h=QK_HEADS).unsqueeze(1).to_broadcast(shape),
                 in1=factors[:, (g % SEQ_GROUPS) * TILES + t].unsqueeze(2).to_broadcast(shape),
                 op=ALU.mult,
             )
-            split = products[:].rearrange("p f (q h a i) -> p f q h a i", q=2, h=HEADS, a=2)
+
+        def join_products(pair, products, qk_out):
+            tiles = slice(2 * pair, 2 * pair + 2)
             nc.gpsimd.tensor_tensor(
-                out=qk_out[:, :, t, :, 0:HALF],
-                in0=split[:, 0, :, :, 0, :],
-                in1=split[:, 1, :, :, 1, :],
+                out=qk_out[:, tiles, :, 0:HALF],
+                in0=products[:, :, 0, :, 0:HALF],
+                in1=products[:, :, 1, :, HALF:TURNED],
                 op=ALU.subtract,
             )
             nc.gpsimd.tensor_tensor(
-                out=qk_out[:, :, t, :, HALF:TURNED],
-                in0=split[:, 0, :, :, 1, :],
-                in1=split[:, 1, :, :, 0, :],
+                out=qk_out[:, tiles, :, HALF:TURNED],
+                in0=products[:, :, 0, :, HALF:TURNED],
+                in1=products[:, :, 1, :, 0:HALF],
                 op=ALU.add,
             )
 
-        def store_pair(g, pair, qk_out, v_out):
+        def store_qk(g, pair, qk_out):
             tiles = slice(2 * pair, 2 * pair + 2)
-            cols = slice(2 * E * pair, 2 * E * (pair + 1))
-            nc.sync.dma_start(
-                out=out_groups[2][g][:, cols], in_=v_out[:, tiles, :].rearrange("p t n -> p (t n)")
-            )
-            for q in range(2):
+            for q, dram in enumerate((q_groups, k_groups)):
                 nc.sync.dma_start(
-                    out=out_groups[q][g][:, cols],
-                    in_=qk_out[:, q, tiles].rearrange("p t h d -> p (t h d)"),
+                    out=dram[g][:, pair_columns(pair)].rearrange("p (t n) -> p t n", t=2),
+                    in_=qk_out[:, tiles, q * HEADS : (q + 1) * HEADS, :].rearrange("p t h d -> p t (h d)"),
                 )
 
+        def store_v(g, pair, v_pair):
+            nc.sync.dma_start(
+                out=v_groups[g][:, pair_columns(pair)], in_=v_pair[:].rearrange("p t n -> p (t n)")
+            )
+
         grouped = stage.tile([P, GROUP * PACK], BF16, align_bytes=64)
-        for pair in range(TILES // 2):
+        for pair in range(PAIRS):
             transpose_x(0, pair, grouped)
-        quantised = quantise(grouped)
+        next_xq = quantise(grouped)
 
         bias_t = psum_turned.tile([P, P], F32, tag="u")
         nc.tensor.transpose(out=bias_t[:], in_=bias_blocks_f32[:], identity=ident[:])
         bias_col = const.tile([P, 2 * BLOCKS], F32)
         nc.vector.tensor_copy(out=bias_col[:], in_=bias_t[:, 0 : 2 * BLOCKS])
 
-        held = {}
         for i in range(GROUPS + 1):
-            if i < GROUPS:
-                codes, scales = quantised
-                feat = stage.tile([P, 2 * BLOCKS, GROUP], F32)
-                qk_out = outs.tile([P, 2, TILES, HEADS, HEAD_DIM], F32)
-                held[i] = (feat, qk_out)
-            if i >= 1:
-                v_out = outs.tile([P, TILES, E], F32)
-            if i + 1 < GROUPS:
+            multiply, finish, prepare = i < GROUPS, i >= 1, i + 1 < GROUPS
+            if finish:
+                old_turned, old_v, old_qk = feat_turned, feat_v, qk_out
+                v_first = outs.tile([P, 2, E], F32)
+            if multiply:
+                xq = next_xq
+                feat_turned = stage.tile([P, BLOCKS, GROUP], F32)
+                feat_v = stage.tile([P, BLOCKS, 2 * P], F32)
+                qk_out = outs.tile([P, TILES, QK_HEADS, HEAD_DIM], F32)
+                v_last = outs.tile([P, 2, E], F32)
+            if prepare:
                 grouped = stage.tile([P, GROUP * PACK], BF16, align_bytes=64)
+
             for step in range(TILES):
-                if i < GROUPS:
-                    feature_major(codes, scales, held[i][0], step)
-                    feature_major(codes, scales, held[i][0], BLOCKS + step)
-                    plain_features(codes, scales, held[i][1], step)
-                if i >= 1:
-                    turned_and_v_features(i - 1, held[i - 1][0], held[i - 1][1], v_out, step)
-                if i + 1 < GROUPS and step < TILES // 2:
+                early = step < PAIRS
+                if multiply:
+                    feature_major(xq, "turned", step, feat_turned)
+                    feature_major(xq, "v", step, feat_v)
+                    plain = psum_plain.tile([P, E], F32)
+                    token_major(xq, "plain", step, plain)
+                    nc.vector.tensor_tensor(
+                        out=qk_out[:, step, :, TURNED:HEAD_DIM],
+                        in0=plain[:].rearrange("p (h j) -> p h j", h=QK_HEADS),
+                        in1=plain_bias,
+                        op=ALU.add,
+                    )
+                    if not early:
+                        v_bank = psum_v.tile([P, E], F32)
+                        token_major(xq, "v", step, v_bank)
+                        nc.scalar.copy(out=v_last[:, step - PAIRS, :], in_=v_bank[:])
+                if finish:
+                    if step % 2 == 0:
+                        products = stage.tile([P, 2, 2, QK_HEADS, TURNED], F32)
+                    u = psum_turned.tile([P, E], F32)
+                    back_to_tokens(old_turned, step, u)
+                    multiply_by_cos_and_sin(i - 1, step, u, products)
+                    if early:
+                        v_bank = psum_v.tile([P, E], F32)
+                        back_to_tokens(old_v, step, v_bank)
+                        nc.scalar.copy(out=v_first[:, step, :], in_=v_bank[:])
+                    if step % 2 == 1:
+                        join_products(step // 2, products, old_qk)
+                if prepare and early:
                     transpose_x(i + 1, step, grouped)
-                if i + 1 < GROUPS and step == TILES // 2:
-                    quantised = quantise(grouped)
-                if i >= 1 and step % 2 == 1:
-                    store_pair(i - 1, step // 2, held[i - 1][1], v_out)
+                if prepare and step == PAIRS:
+                    next_xq = quantise(grouped)
+                if finish and step == 1:
+                    store_v(i - 1, 0, v_first)
+                if finish and step % 2 == 1:
+                    store_qk(i - 1, step // 2, old_qk)
+            if multiply:
+                nc.gpsimd.tensor_tensor(
+                    out=v_last[:],
+                    in0=v_last[:],
+                    in1=v_bias.unsqueeze(1).to_broadcast([P, 2, E]),
+                    op=ALU.add,
+                )
+                store_v(i, 1, v_last)

@@ -26,6 +26,7 @@ GROUP = TILES * P
 GROUPS = BATCH * SEQ // GROUP
 SEQ_GROUPS = SEQ // GROUP
 BLOCKS = E // P
+TURNED_LAG = 2
 
 FLOPS = 2 * BATCH * SEQ * E * 3 * E
 
@@ -40,9 +41,6 @@ def tile_improvedattention_pa_t_kernel(
         out.rearrange("b (sg p t) h d -> (b sg) p (t h d)", sg=SEQ_GROUPS, p=P, t=TILES)
         for out in (out_0, out_1, out_2)
     ]
-
-    def pair_columns(pair):
-        return slice(2 * E * pair, 2 * E * (pair + 1))
 
     with ExitStack() as ctx:
         ctx.enter_context(tc.manual_schedule())
@@ -63,7 +61,7 @@ def tile_improvedattention_pa_t_kernel(
 
         def load_x(g):
             for pair in range(PAIRS):
-                cols = pair_columns(pair)
+                cols = slice(2 * E * pair, 2 * E * (pair + 1))
                 nc.sync.dma_start(out=x_tiles[g][:, cols], in_=x_groups[g][:, cols])
 
         load_x(0)
@@ -73,16 +71,6 @@ def tile_improvedattention_pa_t_kernel(
             out=w_raw[:].bitcast(I32),
             in_=W_qkv_words.rearrange("o p n -> (o p) n").bitcast(I32),
         )
-        bias_blocks = const.tile([P, P], BF16)
-        nc.vector.memset(bias_blocks[:], 0.0)
-        nc.sync.dma_start(
-            out=bias_blocks[0:BLOCKS, :].rearrange("k (h j) -> k h j", j=TURNED),
-            in_=b_qkv[0 : 2 * E].rearrange("(k h c j) -> k h c j", k=BLOCKS, c=2, j=TURNED)[:, :, 0, :],
-        )
-        nc.sync.dma_start(
-            out=bias_blocks[BLOCKS : 2 * BLOCKS, :],
-            in_=b_qkv[2 * E : 3 * E].rearrange("(k c) -> k c", k=BLOCKS),
-        )
         ws_raw = const.tile([P, 3 * E], U8, align_bytes=64)
         nc.vector.memset(ws_raw[:].bitcast(I32), 0)
         scale_rows = W_qkv_scales.rearrange("o q n -> (o q) n")
@@ -91,28 +79,46 @@ def tile_improvedattention_pa_t_kernel(
                 out=ws_raw[32 * quadrant : 32 * quadrant + 4, :].bitcast(I32),
                 in_=scale_rows[4 * quadrant : 4 * quadrant + 4, :].bitcast(I32),
             )
-        bias_rows = const.tile([P, 3 * E], BF16)
-        nc.sync.dma_start(out=bias_rows[:], in_=b_qkv.partition_broadcast(P))
-        load_x(1)
+        qk_bias = b_qkv[0 : 2 * E].rearrange("(k h c j) -> k h c j", k=BLOCKS, c=2, j=TURNED)
+        bias_blocks = const.tile([P, P], BF16)
+        nc.vector.memset(bias_blocks[:], 0.0)
+        nc.sync.dma_start(
+            out=bias_blocks[0:BLOCKS, :].rearrange("k (h j) -> k h j", j=TURNED),
+            in_=qk_bias[:, :, 0, :],
+        )
+        nc.sync.dma_start(
+            out=bias_blocks[BLOCKS : 2 * BLOCKS, :],
+            in_=b_qkv[2 * E : 3 * E].rearrange("(k c) -> k c", k=BLOCKS),
+        )
+        plain_row = const.tile([P, E], BF16)
+        nc.vector.memset(plain_row[:], 0.0)
+        nc.sync.dma_start(
+            out=plain_row[0:1, :].rearrange("o (h j) -> o h j", j=TURNED),
+            in_=b_qkv[0 : 2 * E].rearrange("(o h c j) -> o h c j", o=1, c=2, j=TURNED)[:, :, 1, :],
+        )
+        ones = const.tile([P, P], BF16)
+        nc.vector.memset(ones[:], 1.0)
+
         tables = const.tile([P, 2, SEQ_GROUPS * TILES, TURNED], BF16)
         for which, table in enumerate((cos_tab, sin_tab)):
             nc.sync.dma_start(
                 out=tables[:, which].rearrange("p (sg t) j -> p sg (t j)", sg=SEQ_GROUPS),
                 in_=table.rearrange("(sg p t) j -> p sg (t j)", sg=SEQ_GROUPS, p=P, t=TILES),
             )
-        for g in range(2, GROUPS):
+        for g in range(1, GROUPS):
             load_x(g)
 
         ident = const.tile([P, P], F32)
         make_identity(nc, ident[:])
 
+        cos, sin = tables[:, 0], tables[:, 1]
+        lo, hi = slice(0, HALF), slice(HALF, TURNED)
         factors = const.tile([P, SEQ_GROUPS * TILES, 2, TURNED], BF16)
-        nc.gpsimd.tensor_copy(out=factors[:, :, 0, :], in_=tables[:, 0])
-        nc.gpsimd.tensor_copy(out=factors[:, :, 1, 0:HALF], in_=tables[:, 1, :, HALF:TURNED])
-        nc.gpsimd.tensor_copy(out=factors[:, :, 1, HALF:TURNED], in_=tables[:, 1, :, 0:HALF])
-
-        bias_blocks_f32 = const.tile([P, P], F32)
-        nc.vector.tensor_copy(out=bias_blocks_f32[:], in_=bias_blocks[:])
+        for o, half, table, sign in ((0, lo, cos[:, :, lo], 1.0), (0, hi, sin[:, :, lo], -1.0),
+                                     (1, lo, sin[:, :, hi], 1.0), (1, hi, cos[:, :, hi], 1.0)):
+            nc.gpsimd.tensor_scalar(
+                out=factors[:, :, o, half], in0=table, scalar1=sign, scalar2=0.0, op0=ALU.mult, op1=ALU.add
+            )
 
         w_qk = const.tile([P, 2 * 2 * E], U8, align_bytes=64)
         nc.vector.tensor_copy(
@@ -131,11 +137,8 @@ def tile_improvedattention_pa_t_kernel(
                 "plain": (w_qk, ws_qk, E),
                 "v": (w_raw, ws_raw, 2 * E),
             }[kind]
-            lo = base + first
-            return words[:, 2 * lo : 2 * (lo + count)].bitcast(FP4X4), plane[:, lo : lo + count]
-
-        plain_bias = bias_rows[:, 0 : 2 * E].rearrange("p (h c j) -> p h c j", h=QK_HEADS, c=2)[:, :, 1, :]
-        v_bias = bias_rows[:, 2 * E : 3 * E]
+            start = base + first
+            return words[:, 2 * start : 2 * (start + count)].bitcast(FP4X4), plane[:, start : start + count]
 
         def transpose_x(g, pair, grouped):
             x_words = x_tiles[g][:].bitcast(F32)
@@ -149,7 +152,8 @@ def tile_improvedattention_pa_t_kernel(
                         identity=ident[:],
                     )
             grouped_words = grouped[:].bitcast(F32).rearrange("p (c u) -> p c u", u=2)
-            nc.scalar.copy(
+            copy = nc.scalar.copy if pair == 0 else nc.vector.tensor_copy
+            copy(
                 out=grouped_words[:, 2 * P * pair : 2 * P * (pair + 1), :].rearrange(
                     "p (i c) u -> p i c u", i=2
                 ),
@@ -164,38 +168,44 @@ def tile_improvedattention_pa_t_kernel(
 
         def feature_major(xq, kind, k, feat):
             codes, scales = xq
-            tokens = feat.shape[2]
             w_words, w_plane = weight_columns(kind, k * P, P)
             column = k if kind == "turned" else BLOCKS + k
             acc = psum_feat.tile([P, GROUP], F32)
             nc.tensor.matmul_mx(
-                out=acc[:, 0:tokens],
+                out=acc[:],
                 lhsT=w_words,
                 lhsT_scale=w_plane,
-                rhs=codes[:, 0:tokens].bitcast(FP8X4),
-                rhs_scale=scales[:, 0:tokens],
+                rhs=codes[:].bitcast(FP8X4),
+                rhs_scale=scales[:],
                 start=True,
                 stop=True,
             )
             nc.scalar.activation(
                 out=feat[:, k, :],
-                in_=acc[:, 0:tokens],
+                in_=acc[:],
                 func=IDENTITY,
                 bias=bias_col[:, column : column + 1],
                 scale=1.0,
             )
 
-        def token_major(xq, kind, t, bank):
+        def plain_features(xq, t, qk_out):
             codes, scales = xq
-            w_words, w_plane = weight_columns(kind, 0, E)
+            w_words, w_plane = weight_columns("plain", 0, E)
+            plain = psum_plain.tile([P, E], F32)
             nc.tensor.matmul_mx(
-                out=bank[:],
+                out=plain[:],
                 lhsT=codes[:, t * P : (t + 1) * P].bitcast(FP8X4),
                 lhsT_scale=scales[:, t * P : (t + 1) * P],
                 rhs=w_words,
                 rhs_scale=w_plane,
                 start=True,
                 stop=True,
+            )
+            nc.vector.tensor_tensor(
+                out=qk_out[:, t, :, TURNED:HEAD_DIM],
+                in0=plain[:].rearrange("p (h j) -> p h j", h=QK_HEADS),
+                in1=plain_bias[:].rearrange("p (h j) -> p h j", h=QK_HEADS),
+                op=ALU.add,
             )
 
         def back_to_tokens(feat, t, bank):
@@ -206,109 +216,77 @@ def tile_improvedattention_pa_t_kernel(
                     identity=ident[:],
                 )
 
-        def multiply_by_cos_and_sin(g, t, u, products):
+        def finish_turned(g, t, feat, qk_out):
+            u = psum_turned.tile([P, E], F32)
+            back_to_tokens(feat, t, u)
+            products = outs.tile([P, 2, QK_HEADS, TURNED], F32)
             shape = [P, 2, QK_HEADS, TURNED]
             nc.vector.tensor_tensor(
-                out=products[:, t % 2],
+                out=products[:],
                 in0=u[:].rearrange("p (h j) -> p h j", h=QK_HEADS).unsqueeze(1).to_broadcast(shape),
                 in1=factors[:, (g % SEQ_GROUPS) * TILES + t].unsqueeze(2).to_broadcast(shape),
                 op=ALU.mult,
             )
-
-        def join_products(pair, products, qk_out):
-            tiles = slice(2 * pair, 2 * pair + 2)
+            terms = products[:].rearrange("p o h j -> p h o j")
             nc.gpsimd.tensor_tensor(
-                out=qk_out[:, tiles, :, 0:HALF],
-                in0=products[:, :, 0, :, 0:HALF],
-                in1=products[:, :, 1, :, HALF:TURNED],
-                op=ALU.subtract,
-            )
-            nc.gpsimd.tensor_tensor(
-                out=qk_out[:, tiles, :, HALF:TURNED],
-                in0=products[:, :, 0, :, HALF:TURNED],
-                in1=products[:, :, 1, :, 0:HALF],
+                out=qk_out[:, t, :, 0:TURNED].rearrange("p h (o i) -> p h o i", o=2),
+                in0=terms[:, :, :, lo],
+                in1=terms[:, :, :, hi],
                 op=ALU.add,
             )
-
-        def store_qk(g, pair, qk_out):
-            tiles = slice(2 * pair, 2 * pair + 2)
             for q, dram in enumerate((q_groups, k_groups)):
                 nc.sync.dma_start(
-                    out=dram[g][:, pair_columns(pair)].rearrange("p (t n) -> p t n", t=2),
-                    in_=qk_out[:, tiles, q * HEADS : (q + 1) * HEADS, :].rearrange("p t h d -> p t (h d)"),
+                    out=dram[g][:, t * E : (t + 1) * E],
+                    in_=qk_out[:, t, q * HEADS : (q + 1) * HEADS, :].rearrange("p h d -> p (h d)"),
                 )
 
-        def store_v(g, pair, v_pair):
-            nc.sync.dma_start(
-                out=v_groups[g][:, pair_columns(pair)], in_=v_pair[:].rearrange("p t n -> p (t n)")
-            )
+        def finish_v(g, t, feat, v_out):
+            v_bank = psum_v.tile([P, E], F32)
+            back_to_tokens(feat, t, v_bank)
+            nc.scalar.copy(out=v_out[:, t, :], in_=v_bank[:])
+            if t % 2 == 1:
+                nc.sync.dma_start(
+                    out=v_groups[g][:, (t - 1) * E : (t + 1) * E],
+                    in_=v_out[:, t - 1 : t + 1, :].rearrange("p t n -> p (t n)"),
+                )
 
         grouped = stage.tile([P, GROUP * PACK], BF16, align_bytes=64)
         for pair in range(PAIRS):
             transpose_x(0, pair, grouped)
-        next_xq = quantise(grouped)
+        bias_blocks_f32 = const.tile([P, P], F32)
+        nc.vector.tensor_copy(out=bias_blocks_f32[:], in_=bias_blocks[:])
+        xq = {0: quantise(grouped)}
 
         bias_t = psum_turned.tile([P, P], F32, tag="u")
         nc.tensor.transpose(out=bias_t[:], in_=bias_blocks_f32[:], identity=ident[:])
         bias_col = const.tile([P, 2 * BLOCKS], F32)
         nc.vector.tensor_copy(out=bias_col[:], in_=bias_t[:, 0 : 2 * BLOCKS])
+        bias_bank = psum_plain.tile([P, E], F32, tag="plain")
+        nc.tensor.matmul(out=bias_bank[:], lhsT=ones[:], rhs=plain_row[:], start=True, stop=True)
+        plain_bias = const.tile([P, E], F32)
+        nc.scalar.copy(out=plain_bias[:], in_=bias_bank[:])
 
+        feat_turned, feat_v, qk_outs, v_outs = {}, {}, {}, {}
         for i in range(GROUPS + 1):
-            multiply, finish, prepare = i < GROUPS, i >= 1, i + 1 < GROUPS
-            if finish:
-                old_turned, old_v, old_qk = feat_turned, feat_v, qk_out
-                v_first = outs.tile([P, 2, E], F32)
-            if multiply:
-                xq = next_xq
-                feat_turned = stage.tile([P, BLOCKS, GROUP], F32)
-                feat_v = stage.tile([P, BLOCKS, 2 * P], F32)
-                qk_out = outs.tile([P, TILES, QK_HEADS, HEAD_DIM], F32)
-                v_last = outs.tile([P, 2, E], F32)
-            if prepare:
+            if i < GROUPS:
+                feat_turned[i] = stage.tile([P, BLOCKS, GROUP], F32, name="feat_turned")
+                feat_v[i] = stage.tile([P, BLOCKS, GROUP], F32, name="feat_v")
+                qk_outs[i] = outs.tile([P, TILES, QK_HEADS, HEAD_DIM], F32, name="qk_out")
+                v_outs[i] = outs.tile([P, TILES, E], F32, name="v_out")
+            if i + 1 < GROUPS:
                 grouped = stage.tile([P, GROUP * PACK], BF16, align_bytes=64)
-
             for step in range(TILES):
-                early = step < PAIRS
-                if multiply:
-                    feature_major(xq, "turned", step, feat_turned)
-                    feature_major(xq, "v", step, feat_v)
-                    plain = psum_plain.tile([P, E], F32)
-                    token_major(xq, "plain", step, plain)
-                    nc.vector.tensor_tensor(
-                        out=qk_out[:, step, :, TURNED:HEAD_DIM],
-                        in0=plain[:].rearrange("p (h j) -> p h j", h=QK_HEADS),
-                        in1=plain_bias,
-                        op=ALU.add,
-                    )
-                    if not early:
-                        v_bank = psum_v.tile([P, E], F32)
-                        token_major(xq, "v", step, v_bank)
-                        nc.scalar.copy(out=v_last[:, step - PAIRS, :], in_=v_bank[:])
-                if finish:
-                    if step % 2 == 0:
-                        products = stage.tile([P, 2, 2, QK_HEADS, TURNED], F32)
-                    u = psum_turned.tile([P, E], F32)
-                    back_to_tokens(old_turned, step, u)
-                    multiply_by_cos_and_sin(i - 1, step, u, products)
-                    if early:
-                        v_bank = psum_v.tile([P, E], F32)
-                        back_to_tokens(old_v, step, v_bank)
-                        nc.scalar.copy(out=v_first[:, step, :], in_=v_bank[:])
-                    if step % 2 == 1:
-                        join_products(step // 2, products, old_qk)
-                if prepare and early:
+                if i < GROUPS:
+                    kind, feat = ("turned", feat_turned[i]) if step < PAIRS else ("v", feat_v[i])
+                    for k in (2 * (step % PAIRS), 2 * (step % PAIRS) + 1):
+                        feature_major(xq[i], kind, k, feat)
+                    plain_features(xq[i], step, qk_outs[i])
+                g, t = divmod(TILES * i + step - TURNED_LAG, TILES)
+                if 0 <= g < GROUPS:
+                    finish_turned(g, t, feat_turned[g], qk_outs[g])
+                if i >= 1:
+                    finish_v(i - 1, step, feat_v[i - 1], v_outs[i - 1])
+                if i + 1 < GROUPS and step < PAIRS:
                     transpose_x(i + 1, step, grouped)
-                if prepare and step == PAIRS:
-                    next_xq = quantise(grouped)
-                if finish and step == 1:
-                    store_v(i - 1, 0, v_first)
-                if finish and step % 2 == 1:
-                    store_qk(i - 1, step // 2, old_qk)
-            if multiply:
-                nc.gpsimd.tensor_tensor(
-                    out=v_last[:],
-                    in0=v_last[:],
-                    in1=v_bias.unsqueeze(1).to_broadcast([P, 2, E]),
-                    op=ALU.add,
-                )
-                store_v(i, 1, v_last)
+                if i + 1 < GROUPS and step == PAIRS:
+                    xq[i + 1] = quantise(grouped)

@@ -11,7 +11,6 @@ U8 = mybir.dt.uint8
 FP8X4 = mybir.dt.float8_e4m3fn_x4
 FP4X4 = mybir.dt.float4_e2m1fn_x4
 ALU = mybir.AluOpType
-IDENTITY = mybir.ActivationFunctionType.Identity
 
 P = 128
 PACK = 4
@@ -26,7 +25,7 @@ GROUP = TILES * P
 GROUPS = BATCH * SEQ // GROUP
 SEQ_GROUPS = SEQ // GROUP
 BLOCKS = E // P
-TURNED_LAG = 2
+BLOCK_HEADS = P // TURNED
 
 FLOPS = 2 * BATCH * SEQ * E * 3 * E
 
@@ -51,8 +50,8 @@ def tile_improvedattention_pa_t_kernel(
         psum_x = ctx.enter_context(tc.psum_pool(name="psum_x", bufs=1))
         psum_feat = ctx.enter_context(tc.psum_pool(name="psum_feat", bufs=2))
         psum_plain = ctx.enter_context(tc.psum_pool(name="psum_plain", bufs=1))
-        psum_turned = ctx.enter_context(tc.psum_pool(name="psum_turned", bufs=2))
         psum_v = ctx.enter_context(tc.psum_pool(name="psum_v", bufs=2))
+        psum_r = ctx.enter_context(tc.psum_pool(name="psum_r", bufs=2))
 
         x_tiles = []
         for g in range(GROUPS):
@@ -66,6 +65,12 @@ def tile_improvedattention_pa_t_kernel(
 
         load_x(0)
 
+        tables = const.tile([P, 2, SEQ_GROUPS * TILES, TURNED], BF16)
+        for which, table in enumerate((cos_tab, sin_tab)):
+            nc.sync.dma_start(
+                out=tables[:, which].rearrange("p (sg t) j -> p sg (t j)", sg=SEQ_GROUPS),
+                in_=table.rearrange("(sg p t) j -> p sg (t j)", sg=SEQ_GROUPS, p=P, t=TILES),
+            )
         w_raw = const.tile([P, 2 * 3 * E], U8, align_bytes=64)
         nc.sync.dma_start(
             out=w_raw[:].bitcast(I32),
@@ -86,50 +91,71 @@ def tile_improvedattention_pa_t_kernel(
             out=bias_blocks[0:BLOCKS, :].rearrange("k (h j) -> k h j", j=TURNED),
             in_=qk_bias[:, :, 0, :],
         )
+        bias_rows = const.tile([P, 2, E], BF16)
+        nc.vector.memset(bias_rows[:], 0.0)
         nc.sync.dma_start(
-            out=bias_blocks[BLOCKS : 2 * BLOCKS, :],
-            in_=b_qkv[2 * E : 3 * E].rearrange("(k c) -> k c", k=BLOCKS),
-        )
-        plain_row = const.tile([P, E], BF16)
-        nc.vector.memset(plain_row[:], 0.0)
-        nc.sync.dma_start(
-            out=plain_row[0:1, :].rearrange("o (h j) -> o h j", j=TURNED),
+            out=bias_rows[0:1, 0, :].rearrange("o (h j) -> o h j", j=TURNED),
             in_=b_qkv[0 : 2 * E].rearrange("(o h c j) -> o h c j", o=1, c=2, j=TURNED)[:, :, 1, :],
+        )
+        nc.sync.dma_start(
+            out=bias_rows[0:1, 1, :],
+            in_=b_qkv[2 * E : 3 * E].rearrange("(o n) -> o n", o=1),
         )
         ones = const.tile([P, P], BF16)
         nc.vector.memset(ones[:], 1.0)
-
-        tables = const.tile([P, 2, SEQ_GROUPS * TILES, TURNED], BF16)
-        for which, table in enumerate((cos_tab, sin_tab)):
-            nc.sync.dma_start(
-                out=tables[:, which].rearrange("p (sg t) j -> p sg (t j)", sg=SEQ_GROUPS),
-                in_=table.rearrange("(sg p t) j -> p sg (t j)", sg=SEQ_GROUPS, p=P, t=TILES),
-            )
         for g in range(1, GROUPS):
             load_x(g)
 
         ident = const.tile([P, P], F32)
         make_identity(nc, ident[:])
+        ident_bf = const.tile([P, P], BF16)
+        make_identity(nc, ident_bf[:])
+        swap = const.tile([P, P], F32)
+        ident_halves = ident[:].rearrange("p (a b c) -> p a b c", b=2, c=HALF)
+        swap_halves = swap[:].rearrange("p (a b c) -> p a b c", b=2, c=HALF)
+        for b in range(2):
+            nc.vector.tensor_copy(out=swap_halves[:, :, b, :], in_=ident_halves[:, :, 1 - b, :])
 
         cos, sin = tables[:, 0], tables[:, 1]
         lo, hi = slice(0, HALF), slice(HALF, TURNED)
-        factors = const.tile([P, SEQ_GROUPS * TILES, 2, TURNED], BF16)
-        for o, half, table, sign in ((0, lo, cos[:, :, lo], 1.0), (0, hi, sin[:, :, lo], -1.0),
-                                     (1, lo, sin[:, :, hi], 1.0), (1, hi, cos[:, :, hi], 1.0)):
-            nc.gpsimd.tensor_scalar(
-                out=factors[:, :, o, half], in0=table, scalar1=sign, scalar2=0.0, op0=ALU.mult, op1=ALU.add
-            )
+        factor_rows = const.tile([P, SEQ_GROUPS * TILES, 2, BLOCK_HEADS, TURNED], BF16)
+
+        def make_factor_rows(engine, sg):
+            tiles = slice(sg * TILES, (sg + 1) * TILES)
+            for o, cols, table, sign in ((0, slice(0, TURNED), cos[:, tiles, :], 1.0),
+                                         (1, lo, sin[:, tiles, hi], 1.0), (1, hi, sin[:, tiles, lo], -1.0)):
+                width = cols.stop - cols.start
+                engine.tensor_scalar(
+                    out=factor_rows[:, tiles, o, :, cols],
+                    in0=table.unsqueeze(2).to_broadcast([P, TILES, BLOCK_HEADS, width]),
+                    scalar1=sign, scalar2=0.0, op0=ALU.mult, op1=ALU.add,
+                )
+
+        factors = const.tile([P, SEQ_GROUPS, 2, GROUP], BF16)
+
+        def turn_factors(sg):
+            bank = psum_r.tile([P, 2, TILES, P], BF16, tag="r")
+            for o in range(2):
+                for t in range(TILES):
+                    nc.tensor.transpose(
+                        out=bank[:, o, t, :],
+                        in_=factor_rows[:, sg * TILES + t, o].rearrange("p h i -> p (h i)"),
+                        identity=ident_bf[:],
+                    )
+            nc.scalar.copy(out=factors[:, sg].rearrange("p o c -> p (o c)"), in_=bank[:].rearrange("p o t c -> p (o t c)"))
 
         w_qk = const.tile([P, 2 * 2 * E], U8, align_bytes=64)
-        nc.vector.tensor_copy(
-            out=w_qk[:].bitcast(I32).rearrange("p (c h b) -> p c h b", c=2, h=QK_HEADS),
-            in_=w_raw[:, 0 : 2 * 2 * E].bitcast(I32).rearrange("p (h c b) -> p c h b", h=QK_HEADS, c=2),
-        )
         ws_qk = const.tile([P, 2 * E], U8, align_bytes=64)
-        nc.vector.tensor_copy(
-            out=ws_qk[:].bitcast(I32).rearrange("p (c h b) -> p c h b", c=2, h=QK_HEADS),
-            in_=ws_raw[:, 0 : 2 * E].bitcast(I32).rearrange("p (h c b) -> p c h b", h=QK_HEADS, c=2),
-        )
+
+        def sort_weight_columns():
+            nc.vector.tensor_copy(
+                out=w_qk[:].bitcast(I32).rearrange("p (c h b) -> p c h b", c=2, h=QK_HEADS),
+                in_=w_raw[:, 0 : 2 * 2 * E].bitcast(I32).rearrange("p (h c b) -> p c h b", h=QK_HEADS, c=2),
+            )
+            nc.vector.tensor_copy(
+                out=ws_qk[:].bitcast(I32).rearrange("p (c h b) -> p c h b", c=2, h=QK_HEADS),
+                in_=ws_raw[:, 0 : 2 * E].bitcast(I32).rearrange("p (h c b) -> p c h b", h=QK_HEADS, c=2),
+            )
 
         def weight_columns(kind, first, count):
             words, plane, base = {
@@ -152,8 +178,7 @@ def tile_improvedattention_pa_t_kernel(
                         identity=ident[:],
                     )
             grouped_words = grouped[:].bitcast(F32).rearrange("p (c u) -> p c u", u=2)
-            copy = nc.scalar.copy if pair == 0 else nc.vector.tensor_copy
-            copy(
+            nc.scalar.copy(
                 out=grouped_words[:, 2 * P * pair : 2 * P * (pair + 1), :].rearrange(
                     "p (i c) u -> p i c u", i=2
                 ),
@@ -166,10 +191,9 @@ def tile_improvedattention_pa_t_kernel(
             nc.vector.quantize_mx(out=codes[:].bitcast(FP8X4), scales=scales[:], in_=grouped[:])
             return codes, scales
 
-        def feature_major(xq, kind, k, feat):
+        def turned_block(xq, g, k, products):
             codes, scales = xq
-            w_words, w_plane = weight_columns(kind, k * P, P)
-            column = k if kind == "turned" else BLOCKS + k
+            w_words, w_plane = weight_columns("turned", k * P, P)
             acc = psum_feat.tile([P, GROUP], F32)
             nc.tensor.matmul_mx(
                 out=acc[:],
@@ -180,20 +204,21 @@ def tile_improvedattention_pa_t_kernel(
                 start=True,
                 stop=True,
             )
-            nc.scalar.activation(
-                out=feat[:, k, :],
-                in_=acc[:],
-                func=IDENTITY,
-                bias=bias_col[:, column : column + 1],
-                scale=1.0,
+            nc.vector.scalar_tensor_tensor(
+                out=products[:, k],
+                in0=acc[:].unsqueeze(1).to_broadcast([P, 2, GROUP]),
+                scalar=bias_col[:, k : k + 1],
+                in1=factors[:, g % SEQ_GROUPS],
+                op0=ALU.add,
+                op1=ALU.mult,
             )
 
-        def plain_features(xq, t, qk_out):
+        def token_major(xq, kind, t, pool):
             codes, scales = xq
-            w_words, w_plane = weight_columns("plain", 0, E)
-            plain = psum_plain.tile([P, E], F32)
+            w_words, w_plane = weight_columns(kind, 0, E)
+            bank = pool.tile([P, E], F32, name=kind)
             nc.tensor.matmul_mx(
-                out=plain[:],
+                out=bank[:],
                 lhsT=codes[:, t * P : (t + 1) * P].bitcast(FP8X4),
                 lhsT_scale=scales[:, t * P : (t + 1) * P],
                 rhs=w_words,
@@ -201,92 +226,110 @@ def tile_improvedattention_pa_t_kernel(
                 start=True,
                 stop=True,
             )
+            return bank
+
+        def plain_features(xq, t, qk_out):
+            plain = token_major(xq, "plain", t, psum_plain)
             nc.vector.tensor_tensor(
-                out=qk_out[:, t, :, TURNED:HEAD_DIM],
-                in0=plain[:].rearrange("p (h j) -> p h j", h=QK_HEADS),
-                in1=plain_bias[:].rearrange("p (h j) -> p h j", h=QK_HEADS),
+                out=qk_out[:, :, t, :, TURNED:HEAD_DIM],
+                in0=plain[:].rearrange("p (q h j) -> p q h j", q=2, h=HEADS),
+                in1=free_bias[:, 0, :].rearrange("p (q h j) -> p q h j", q=2, h=HEADS),
                 op=ALU.add,
             )
 
-        def back_to_tokens(feat, t, bank):
-            for k in range(BLOCKS):
-                nc.tensor.transpose(
-                    out=bank[:, k * P : (k + 1) * P],
-                    in_=feat[:, k, t * P : (t + 1) * P],
-                    identity=ident[:],
-                )
+        def v_features(xq, t, v_raw):
+            v_bank = token_major(xq, "v", t, psum_v)
+            nc.scalar.copy(out=v_raw[:, t, :], in_=v_bank[:])
 
-        def finish_turned(g, t, feat, qk_out):
-            u = psum_turned.tile([P, E], F32)
-            back_to_tokens(feat, t, u)
-            products = outs.tile([P, 2, QK_HEADS, TURNED], F32)
-            shape = [P, 2, QK_HEADS, TURNED]
-            nc.vector.tensor_tensor(
-                out=products[:],
-                in0=u[:].rearrange("p (h j) -> p h j", h=QK_HEADS).unsqueeze(1).to_broadcast(shape),
-                in1=factors[:, (g % SEQ_GROUPS) * TILES + t].unsqueeze(2).to_broadcast(shape),
-                op=ALU.mult,
-            )
-            terms = products[:].rearrange("p o h j -> p h o j")
+        def finish_v(g, pair, v_raw, v_out):
+            tiles = slice(2 * pair, 2 * pair + 2)
             nc.gpsimd.tensor_tensor(
-                out=qk_out[:, t, :, 0:TURNED].rearrange("p h (o i) -> p h o i", o=2),
-                in0=terms[:, :, :, lo],
-                in1=terms[:, :, :, hi],
+                out=v_out[:, tiles, :],
+                in0=v_raw[:, tiles, :],
+                in1=free_bias[:, 1, :].unsqueeze(1).to_broadcast([P, 2, E]),
                 op=ALU.add,
             )
+            nc.sync.dma_start(
+                out=v_groups[g][:, 2 * pair * E : (2 * pair + 2) * E],
+                in_=v_out[:, tiles, :].rearrange("p t n -> p (t n)"),
+            )
+
+        def finish_turned(t, products, qk_out):
+            r = psum_r.tile([P, E], F32)
+            for k in range(BLOCKS):
+                for o, moving in enumerate((ident, swap)):
+                    nc.tensor.matmul(
+                        out=r[:, k * P : (k + 1) * P],
+                        lhsT=products[:, k, o, t * P : (t + 1) * P],
+                        rhs=moving[:],
+                        is_transpose=True,
+                        start=(o == 0),
+                        stop=(o == 1),
+                    )
+            nc.scalar.copy(
+                out=qk_out[:, :, t, :, 0:TURNED],
+                in_=r[:].rearrange("p (q h j) -> p q h j", q=2, h=HEADS),
+            )
+
+        def store_qk(g, pair, qk_out):
             for q, dram in enumerate((q_groups, k_groups)):
                 nc.sync.dma_start(
-                    out=dram[g][:, t * E : (t + 1) * E],
-                    in_=qk_out[:, t, q * HEADS : (q + 1) * HEADS, :].rearrange("p h d -> p (h d)"),
+                    out=dram[g][:, 2 * pair * E : (2 * pair + 2) * E],
+                    in_=qk_out[:, q, 2 * pair : 2 * pair + 2].rearrange("p t h d -> p (t h d)"),
                 )
 
-        def finish_v(g, t, feat, v_out):
-            v_bank = psum_v.tile([P, E], F32)
-            back_to_tokens(feat, t, v_bank)
-            nc.scalar.copy(out=v_out[:, t, :], in_=v_bank[:])
-            if t % 2 == 1:
-                nc.sync.dma_start(
-                    out=v_groups[g][:, (t - 1) * E : (t + 1) * E],
-                    in_=v_out[:, t - 1 : t + 1, :].rearrange("p t n -> p (t n)"),
-                )
-
-        grouped = stage.tile([P, GROUP * PACK], BF16, align_bytes=64)
+        grouped = {0: stage.tile([P, GROUP * PACK], BF16, align_bytes=64, name="grouped")}
         for pair in range(PAIRS):
-            transpose_x(0, pair, grouped)
+            transpose_x(0, pair, grouped[0])
+        make_factor_rows(nc.vector, 0)
+        for sg in range(1, SEQ_GROUPS):
+            make_factor_rows(nc.gpsimd, sg)
+        turn_factors(0)
+        sort_weight_columns()
         bias_blocks_f32 = const.tile([P, P], F32)
         nc.vector.tensor_copy(out=bias_blocks_f32[:], in_=bias_blocks[:])
-        xq = {0: quantise(grouped)}
+        xq = {0: quantise(grouped[0])}
 
-        bias_t = psum_turned.tile([P, P], F32, tag="u")
+        bias_t = psum_plain.tile([P, P], F32, tag="plain")
         nc.tensor.transpose(out=bias_t[:], in_=bias_blocks_f32[:], identity=ident[:])
-        bias_col = const.tile([P, 2 * BLOCKS], F32)
-        nc.vector.tensor_copy(out=bias_col[:], in_=bias_t[:, 0 : 2 * BLOCKS])
-        bias_bank = psum_plain.tile([P, E], F32, tag="plain")
-        nc.tensor.matmul(out=bias_bank[:], lhsT=ones[:], rhs=plain_row[:], start=True, stop=True)
-        plain_bias = const.tile([P, E], F32)
-        nc.scalar.copy(out=plain_bias[:], in_=bias_bank[:])
+        bias_col = const.tile([P, BLOCKS], F32)
+        nc.vector.tensor_copy(out=bias_col[:], in_=bias_t[:, 0:BLOCKS])
+        free_bias = const.tile([P, 2, E], F32)
+        for which in range(2):
+            bias_bank = psum_v.tile([P, E], F32, tag="v")
+            nc.tensor.matmul(out=bias_bank[:], lhsT=ones[:], rhs=bias_rows[:, which, :], start=True, stop=True)
+            nc.scalar.copy(out=free_bias[:, which, :], in_=bias_bank[:])
+        grouped[1] = stage.tile([P, GROUP * PACK], BF16, align_bytes=64, name="grouped")
+        transpose_x(1, 0, grouped[1])
 
-        feat_turned, feat_v, qk_outs, v_outs = {}, {}, {}, {}
+        products, qk_outs, v_raws, v_outs = {}, {}, {}, {}
         for i in range(GROUPS + 1):
             if i < GROUPS:
-                feat_turned[i] = stage.tile([P, BLOCKS, GROUP], F32, name="feat_turned")
-                feat_v[i] = stage.tile([P, BLOCKS, GROUP], F32, name="feat_v")
-                qk_outs[i] = outs.tile([P, TILES, QK_HEADS, HEAD_DIM], F32, name="qk_out")
+                products[i] = stage.tile([P, BLOCKS, 2, GROUP], F32, name="products")
+                qk_outs[i] = outs.tile([P, 2, TILES, HEADS, HEAD_DIM], F32, name="qk_out")
+                v_raws[i] = stage.tile([P, TILES, E], F32, name="v_raw")
                 v_outs[i] = outs.tile([P, TILES, E], F32, name="v_out")
-            if i + 1 < GROUPS:
-                grouped = stage.tile([P, GROUP * PACK], BF16, align_bytes=64)
-            for step in range(TILES):
+            for half in range(PAIRS):
+                a, b = 2 * half, 2 * half + 1
                 if i < GROUPS:
-                    kind, feat = ("turned", feat_turned[i]) if step < PAIRS else ("v", feat_v[i])
-                    for k in (2 * (step % PAIRS), 2 * (step % PAIRS) + 1):
-                        feature_major(xq[i], kind, k, feat)
-                    plain_features(xq[i], step, qk_outs[i])
-                g, t = divmod(TILES * i + step - TURNED_LAG, TILES)
-                if 0 <= g < GROUPS:
-                    finish_turned(g, t, feat_turned[g], qk_outs[g])
+                    plain_features(xq[i], a, qk_outs[i])
+                    turned_block(xq[i], i, a, products[i])
+                    v_features(xq[i], a, v_raws[i])
+                    v_features(xq[i], b, v_raws[i])
+                    if half == 1 and i + 1 < GROUPS:
+                        xq[i + 1] = quantise(grouped[i + 1])
+                    plain_features(xq[i], b, qk_outs[i])
+                    turned_block(xq[i], i, b, products[i])
+                    finish_v(i, half, v_raws[i], v_outs[i])
                 if i >= 1:
-                    finish_v(i - 1, step, feat_v[i - 1], v_outs[i - 1])
-                if i + 1 < GROUPS and step < PAIRS:
-                    transpose_x(i + 1, step, grouped)
-                if i + 1 < GROUPS and step == PAIRS:
-                    xq[i + 1] = quantise(grouped)
+                    finish_turned(a, products[i - 1], qk_outs[i - 1])
+                    finish_turned(b, products[i - 1], qk_outs[i - 1])
+                    store_qk(i - 1, half, qk_outs[i - 1])
+                if i == 0:
+                    for sg in ((1, 2), (3,))[half]:
+                        turn_factors(sg)
+                if half == 0 and i + 1 < GROUPS:
+                    transpose_x(i + 1, 1, grouped[i + 1])
+                if half == 1 and i + 2 < GROUPS:
+                    grouped[i + 2] = stage.tile([P, GROUP * PACK], BF16, align_bytes=64, name="grouped")
+                    transpose_x(i + 2, 0, grouped[i + 2])

@@ -256,15 +256,15 @@ def tile_improvedattention_pa_t_kernel(
 
         def finish_turned(t, products, qk_out):
             r = psum_r.tile([P, E], F32)
-            for k in range(BLOCKS):
-                for o, moving in enumerate((ident, swap)):
+            for o, moving in enumerate((ident, swap)):
+                for k in range(BLOCKS):
                     nc.tensor.matmul(
                         out=r[:, k * P : (k + 1) * P],
                         lhsT=products[:, k, o, t * P : (t + 1) * P],
                         rhs=moving[:],
                         is_transpose=True,
-                        start=(o == 0),
-                        stop=(o == 1),
+                        start=(o == 0 and k == 0),
+                        stop=(o == 1 and k == BLOCKS - 1),
                     )
             nc.scalar.copy(
                 out=qk_out[:, :, t, :, 0:TURNED],

@@ -166,17 +166,27 @@ def tile_improvedattention_pa_t_kernel(
             start = base + first
             return words[:, 2 * start : 2 * (start + count)].bitcast(FP4X4), plane[:, start : start + count]
 
+        sorted_words = {}
+
+        def sort_x_words(g, pair):
+            x_words = x_tiles[g][:].bitcast(F32)
+            sorted_words[g, pair] = stage.tile([P, 2, 2, P], F32, name="sorted_words")
+            nc.scalar.copy(
+                out=sorted_words[g, pair][:],
+                in_=x_words[:, pair * E : (pair + 1) * E].rearrange("p (i c u) -> p i u c", i=2, u=2),
+            )
+
         def transpose_x(g, pair, grouped):
             x_words = x_tiles[g][:].bitcast(F32)
             xt = psum_x.tile([P, 2, 2, P], F32)
             for i in range(2):
                 first = (2 * pair + i) * (E // 2)
                 for u in range(2):
-                    nc.tensor.transpose(
-                        out=xt[:, i, u, :],
-                        in_=x_words[:, first + u : first + E // 2 : 2],
-                        identity=ident[:],
-                    )
+                    if (g, pair) in sorted_words:
+                        words = sorted_words[g, pair][:, i, u, :]
+                    else:
+                        words = x_words[:, first + u : first + E // 2 : 2]
+                    nc.tensor.transpose(out=xt[:, i, u, :], in_=words, identity=ident[:])
             grouped_words = grouped[:].bitcast(F32).rearrange("p (c u) -> p c u", u=2)
             nc.scalar.copy(
                 out=grouped_words[:, 2 * P * pair : 2 * P * (pair + 1), :].rearrange(
@@ -301,6 +311,7 @@ def tile_improvedattention_pa_t_kernel(
             nc.scalar.copy(out=free_bias[:, which, :], in_=bias_bank[:])
         grouped[1] = stage.tile([P, GROUP * PACK], BF16, align_bytes=64, name="grouped")
         transpose_x(1, 0, grouped[1])
+        sort_x_words(1, 1)
 
         products, qk_outs, v_raws, v_outs = {}, {}, {}, {}
         for i in range(GROUPS + 1):
@@ -321,6 +332,8 @@ def tile_improvedattention_pa_t_kernel(
                     plain_features(xq[i], b, qk_outs[i])
                     turned_block(xq[i], i, b, products[i])
                     finish_v(i, half, v_raws[i], v_outs[i])
+                if i + 2 < GROUPS:
+                    sort_x_words(i + 2, half)
                 if i >= 1:
                     finish_turned(a, products[i - 1], qk_outs[i - 1])
                     finish_turned(b, products[i - 1], qk_outs[i - 1])

@@ -47,9 +47,8 @@ def tile_improvedattention_pa_t_kernel(
         x_pool = ctx.enter_context(tc.tile_pool(name="x_pool", bufs=GROUPS))
         stage = ctx.enter_context(tc.tile_pool(name="stage", bufs=2))
         outs = ctx.enter_context(tc.tile_pool(name="outs", bufs=3))
-        psum_x = ctx.enter_context(tc.psum_pool(name="psum_x", bufs=1))
+        psum_px = ctx.enter_context(tc.psum_pool(name="psum_px", bufs=2))
         psum_feat = ctx.enter_context(tc.psum_pool(name="psum_feat", bufs=2))
-        psum_plain = ctx.enter_context(tc.psum_pool(name="psum_plain", bufs=1))
         psum_v = ctx.enter_context(tc.psum_pool(name="psum_v", bufs=2))
         psum_r = ctx.enter_context(tc.psum_pool(name="psum_r", bufs=2))
 
@@ -178,7 +177,7 @@ def tile_improvedattention_pa_t_kernel(
 
         def transpose_x(g, pair, grouped):
             x_words = x_tiles[g][:].bitcast(F32)
-            xt = psum_x.tile([P, 2, 2, P], F32)
+            xt = psum_px.tile([P, 2, 2, P], F32, tag="px")
             for i in range(2):
                 first = (2 * pair + i) * (E // 2)
                 for u in range(2):
@@ -223,10 +222,10 @@ def tile_improvedattention_pa_t_kernel(
                 op1=ALU.mult,
             )
 
-        def token_major(xq, kind, t, pool):
+        def token_major(xq, kind, t, pool, tag):
             codes, scales = xq
             w_words, w_plane = weight_columns(kind, 0, E)
-            bank = pool.tile([P, E], F32, name=kind)
+            bank = pool.tile([P, E], F32, tag=tag)
             nc.tensor.matmul_mx(
                 out=bank[:],
                 lhsT=codes[:, t * P : (t + 1) * P].bitcast(FP8X4),
@@ -239,7 +238,7 @@ def tile_improvedattention_pa_t_kernel(
             return bank
 
         def plain_features(xq, t, qk_out):
-            plain = token_major(xq, "plain", t, psum_plain)
+            plain = token_major(xq, "plain", t, psum_px, "px")
             nc.vector.tensor_tensor(
                 out=qk_out[:, :, t, :, TURNED:HEAD_DIM],
                 in0=plain[:].rearrange("p (q h j) -> p q h j", q=2, h=HEADS),
@@ -248,7 +247,7 @@ def tile_improvedattention_pa_t_kernel(
             )
 
         def v_features(xq, t, v_raw):
-            v_bank = token_major(xq, "v", t, psum_v)
+            v_bank = token_major(xq, "v", t, psum_v, "v")
             nc.scalar.copy(out=v_raw[:, t, :], in_=v_bank[:])
 
         def finish_v(g, pair, v_raw, v_out):
@@ -300,7 +299,7 @@ def tile_improvedattention_pa_t_kernel(
         nc.vector.tensor_copy(out=bias_blocks_f32[:], in_=bias_blocks[:])
         xq = {0: quantise(grouped[0])}
 
-        bias_t = psum_plain.tile([P, P], F32, tag="plain")
+        bias_t = psum_px.tile([P, P], F32, tag="px")
         nc.tensor.transpose(out=bias_t[:], in_=bias_blocks_f32[:], identity=ident[:])
         bias_col = const.tile([P, BLOCKS], F32)
         nc.vector.tensor_copy(out=bias_col[:], in_=bias_t[:, 0:BLOCKS])
@@ -334,6 +333,11 @@ def tile_improvedattention_pa_t_kernel(
                     finish_v(i, half, v_raws[i], v_outs[i])
                 if i + 2 < GROUPS:
                     sort_x_words(i + 2, half)
+                if half == 0 and i + 1 < GROUPS:
+                    transpose_x(i + 1, 1, grouped[i + 1])
+                if half == 1 and i + 2 < GROUPS:
+                    grouped[i + 2] = stage.tile([P, GROUP * PACK], BF16, align_bytes=64, name="grouped")
+                    transpose_x(i + 2, 0, grouped[i + 2])
                 if i >= 1:
                     finish_turned(a, products[i - 1], qk_outs[i - 1])
                     finish_turned(b, products[i - 1], qk_outs[i - 1])
@@ -341,8 +345,3 @@ def tile_improvedattention_pa_t_kernel(
                 if i == 0:
                     for sg in ((1, 2), (3,))[half]:
                         turn_factors(sg)
-                if half == 0 and i + 1 < GROUPS:
-                    transpose_x(i + 1, 1, grouped[i + 1])
-                if half == 1 and i + 2 < GROUPS:
-                    grouped[i + 2] = stage.tile([P, GROUP * PACK], BF16, align_bytes=64, name="grouped")
-                    transpose_x(i + 2, 0, grouped[i + 2])

@@ -64,17 +64,6 @@ def tile_improvedattention_pa_t_kernel(
 
         load_x(0)
 
-        tables = const.tile([P, 2, SEQ_GROUPS * TILES, TURNED], BF16)
-        for which, table in enumerate((cos_tab, sin_tab)):
-            nc.sync.dma_start(
-                out=tables[:, which].rearrange("p (sg t) j -> p sg (t j)", sg=SEQ_GROUPS),
-                in_=table.rearrange("(sg p t) j -> p sg (t j)", sg=SEQ_GROUPS, p=P, t=TILES),
-            )
-        w_raw = const.tile([P, 2 * 3 * E], U8, align_bytes=64)
-        nc.sync.dma_start(
-            out=w_raw[:].bitcast(I32),
-            in_=W_qkv_words.rearrange("o p n -> (o p) n").bitcast(I32),
-        )
         ws_raw = const.tile([P, 3 * E], U8, align_bytes=64)
         nc.vector.memset(ws_raw[:].bitcast(I32), 0)
         scale_rows = W_qkv_scales.rearrange("o q n -> (o q) n")
@@ -99,6 +88,17 @@ def tile_improvedattention_pa_t_kernel(
         nc.sync.dma_start(
             out=bias_rows[0:1, 1, :],
             in_=b_qkv[2 * E : 3 * E].rearrange("(o n) -> o n", o=1),
+        )
+        tables = const.tile([P, 2, SEQ_GROUPS * TILES, TURNED], BF16)
+        for which, table in enumerate((cos_tab, sin_tab)):
+            nc.sync.dma_start(
+                out=tables[:, which].rearrange("p (sg t) j -> p sg (t j)", sg=SEQ_GROUPS),
+                in_=table.rearrange("(sg p t) j -> p sg (t j)", sg=SEQ_GROUPS, p=P, t=TILES),
+            )
+        w_raw = const.tile([P, 2 * 3 * E], U8, align_bytes=64)
+        nc.sync.dma_start(
+            out=w_raw[:].bitcast(I32),
+            in_=W_qkv_words.rearrange("o p n -> (o p) n").bitcast(I32),
         )
         ones = const.tile([P, P], BF16)
         nc.vector.memset(ones[:], 1.0)
@@ -146,11 +146,13 @@ def tile_improvedattention_pa_t_kernel(
         w_qk = const.tile([P, 2 * 2 * E], U8, align_bytes=64)
         ws_qk = const.tile([P, 2 * E], U8, align_bytes=64)
 
-        def sort_weight_columns():
+        def sort_weight_words():
             nc.vector.tensor_copy(
                 out=w_qk[:].bitcast(I32).rearrange("p (c h b) -> p c h b", c=2, h=QK_HEADS),
                 in_=w_raw[:, 0 : 2 * 2 * E].bitcast(I32).rearrange("p (h c b) -> p c h b", h=QK_HEADS, c=2),
             )
+
+        def sort_weight_scales():
             nc.vector.tensor_copy(
                 out=ws_qk[:].bitcast(I32).rearrange("p (c h b) -> p c h b", c=2, h=QK_HEADS),
                 in_=ws_raw[:, 0 : 2 * E].bitcast(I32).rearrange("p (h c b) -> p c h b", h=QK_HEADS, c=2),
@@ -258,9 +260,11 @@ def tile_improvedattention_pa_t_kernel(
                 in1=free_bias[:, 1, :].unsqueeze(1).to_broadcast([P, 2, E]),
                 op=ALU.add,
             )
+
+        def store_v(g, pair, v_out):
             nc.sync.dma_start(
                 out=v_groups[g][:, 2 * pair * E : (2 * pair + 2) * E],
-                in_=v_out[:, tiles, :].rearrange("p t n -> p (t n)"),
+                in_=v_out[:, 2 * pair : 2 * pair + 2, :].rearrange("p t n -> p (t n)"),
             )
 
         def finish_turned(t, products, qk_out):
@@ -290,24 +294,24 @@ def tile_improvedattention_pa_t_kernel(
         grouped = {0: stage.tile([P, GROUP * PACK], BF16, align_bytes=64, name="grouped")}
         for pair in range(PAIRS):
             transpose_x(0, pair, grouped[0])
-        make_factor_rows(nc.vector, 0)
-        for sg in range(1, SEQ_GROUPS):
-            make_factor_rows(nc.gpsimd, sg)
-        turn_factors(0)
-        sort_weight_columns()
         bias_blocks_f32 = const.tile([P, P], F32)
         nc.vector.tensor_copy(out=bias_blocks_f32[:], in_=bias_blocks[:])
-        xq = {0: quantise(grouped[0])}
-
-        bias_t = psum_px.tile([P, P], F32, tag="px")
-        nc.tensor.transpose(out=bias_t[:], in_=bias_blocks_f32[:], identity=ident[:])
-        bias_col = const.tile([P, BLOCKS], F32)
-        nc.vector.tensor_copy(out=bias_col[:], in_=bias_t[:, 0:BLOCKS])
         free_bias = const.tile([P, 2, E], F32)
         for which in range(2):
             bias_bank = psum_v.tile([P, E], F32, tag="v")
             nc.tensor.matmul(out=bias_bank[:], lhsT=ones[:], rhs=bias_rows[:, which, :], start=True, stop=True)
             nc.scalar.copy(out=free_bias[:, which, :], in_=bias_bank[:])
+        bias_t = psum_r.tile([P, P], F32, tag="r")
+        nc.tensor.transpose(out=bias_t[:], in_=bias_blocks_f32[:], identity=ident[:])
+        make_factor_rows(nc.vector, 0)
+        for sg in range(1, SEQ_GROUPS):
+            make_factor_rows(nc.gpsimd, sg)
+        turn_factors(0)
+        sort_weight_scales()
+        sort_weight_words()
+        xq = {0: quantise(grouped[0])}
+        bias_col = const.tile([P, BLOCKS], F32)
+        nc.vector.tensor_copy(out=bias_col[:], in_=bias_t[:, 0:BLOCKS])
         grouped[1] = stage.tile([P, GROUP * PACK], BF16, align_bytes=64, name="grouped")
         transpose_x(1, 0, grouped[1])
         sort_x_words(1, 1)
@@ -342,6 +346,8 @@ def tile_improvedattention_pa_t_kernel(
                     finish_turned(a, products[i - 1], qk_outs[i - 1])
                     finish_turned(b, products[i - 1], qk_outs[i - 1])
                     store_qk(i - 1, half, qk_outs[i - 1])
+                if i < GROUPS:
+                    store_v(i, half, v_outs[i])
                 if i == 0:
-                    for sg in ((1, 2), (3,))[half]:
+                    for sg in ((1,), (2, 3))[half]:
                         turn_factors(sg)

@@ -284,11 +284,11 @@ def tile_improvedattention_pa_t_kernel(
                 in_=r[:].rearrange("p (q h j) -> p q h j", q=2, h=HEADS),
             )
 
-        def store_qk(g, pair, qk_out):
+        def store_qk(g, first, count, qk_out):
             for q, dram in enumerate((q_groups, k_groups)):
                 nc.sync.dma_start(
-                    out=dram[g][:, 2 * pair * E : (2 * pair + 2) * E],
-                    in_=qk_out[:, q, 2 * pair : 2 * pair + 2].rearrange("p t h d -> p (t h d)"),
+                    out=dram[g][:, first * E : (first + count) * E],
+                    in_=qk_out[:, q, first : first + count].rearrange("p t h d -> p (t h d)"),
                 )
 
         grouped = {0: stage.tile([P, GROUP * PACK], BF16, align_bytes=64, name="grouped")}
@@ -344,8 +344,13 @@ def tile_improvedattention_pa_t_kernel(
                     transpose_x(i + 2, 0, grouped[i + 2])
                 if i >= 1:
                     finish_turned(a, products[i - 1], qk_outs[i - 1])
+                    if i == GROUPS:
+                        store_qk(i - 1, a, 1, qk_outs[i - 1])
                     finish_turned(b, products[i - 1], qk_outs[i - 1])
-                    store_qk(i - 1, half, qk_outs[i - 1])
+                    if i == GROUPS:
+                        store_qk(i - 1, b, 1, qk_outs[i - 1])
+                    else:
+                        store_qk(i - 1, a, 2, qk_outs[i - 1])
                 if i < GROUPS:
                     store_v(i, half, v_outs[i])
                 if i == 0:

from contextlib import ExitStack

import concourse.mybir as mybir
from concourse.masks import make_identity

F32 = mybir.dt.float32
BF16 = mybir.dt.bfloat16
I32 = mybir.dt.int32
U32 = mybir.dt.uint32
U8 = mybir.dt.uint8
FP8X4 = mybir.dt.float8_e4m3fn_x4
FP4X4 = mybir.dt.float4_e2m1fn_x4
ALU = mybir.AluOpType

P = 128
PACK = 4
BATCH, SEQ, HEADS, HEAD_DIM = 2, 2048, 8, 64
E = HEADS * HEAD_DIM
TURNED = HEAD_DIM // 2
HALF = TURNED // 2
QK_HEADS = 2 * HEADS
TILES = 4
PAIRS = TILES // 2
GROUP = TILES * P
GROUPS = BATCH * SEQ // GROUP
SEQ_GROUPS = SEQ // GROUP
BLOCKS = E // P
BLOCK_HEADS = P // TURNED

FLOPS = 2 * BATCH * SEQ * E * 3 * E


def tile_improvedattention_pa_t_kernel(
    tc, x, W_qkv_words, W_qkv_scales, b_qkv, sin_tab, cos_tab, out_0, out_1, out_2
):
    nc = tc.nc

    x_groups = x.rearrange("b (sg p t) k -> (b sg) p (t k)", sg=SEQ_GROUPS, p=P, t=TILES)
    q_groups, k_groups, v_groups = [
        out.rearrange("b (sg p t) h d -> (b sg) p (t h d)", sg=SEQ_GROUPS, p=P, t=TILES)
        for out in (out_0, out_1, out_2)
    ]

    with ExitStack() as ctx:
        ctx.enter_context(tc.manual_schedule())
        const = ctx.enter_context(tc.tile_pool(name="const", bufs=1))
        x_pool = ctx.enter_context(tc.tile_pool(name="x_pool", bufs=GROUPS))
        stage = ctx.enter_context(tc.tile_pool(name="stage", bufs=2))
        outs = ctx.enter_context(tc.tile_pool(name="outs", bufs=3))
        psum_px = ctx.enter_context(tc.psum_pool(name="psum_px", bufs=2))
        psum_feat = ctx.enter_context(tc.psum_pool(name="psum_feat", bufs=2))
        psum_v = ctx.enter_context(tc.psum_pool(name="psum_v", bufs=2))
        psum_r = ctx.enter_context(tc.psum_pool(name="psum_r", bufs=2))

        x_tiles = []
        for g in range(GROUPS):
            x_sb = x_pool.tile([P, TILES * E], BF16)
            x_tiles.append(x_sb)

        def load_x(g):
            for pair in range(PAIRS):
                cols = slice(2 * E * pair, 2 * E * (pair + 1))
                nc.sync.dma_start(out=x_tiles[g][:, cols], in_=x_groups[g][:, cols])

        load_x(0)

        ws_raw = const.tile([P, 3 * E], U8, align_bytes=64)
        nc.vector.memset(ws_raw[:].bitcast(I32), 0)
        scale_rows = W_qkv_scales.rearrange("o q n -> (o q) n")
        for quadrant in range(4):
            nc.sync.dma_start(
                out=ws_raw[32 * quadrant : 32 * quadrant + 4, :].bitcast(I32),
                in_=scale_rows[4 * quadrant : 4 * quadrant + 4, :].bitcast(I32),
            )
        qk_bias = b_qkv[0 : 2 * E].rearrange("(k h c j) -> k h c j", k=BLOCKS, c=2, j=TURNED)
        bias_blocks = const.tile([P, P], BF16)
        nc.vector.memset(bias_blocks[:], 0.0)
        nc.sync.dma_start(
            out=bias_blocks[0:BLOCKS, :].rearrange("k (h j) -> k h j", j=TURNED),
            in_=qk_bias[:, :, 0, :],
        )
        bias_rows = const.tile([P, 2, E], BF16)
        nc.vector.memset(bias_rows[:], 0.0)
        nc.sync.dma_start(
            out=bias_rows[0:1, 0, :].rearrange("o (h j) -> o h j", j=TURNED),
            in_=b_qkv[0 : 2 * E].rearrange("(o h c j) -> o h c j", o=1, c=2, j=TURNED)[:, :, 1, :],
        )
        nc.sync.dma_start(
            out=bias_rows[0:1, 1, :],
            in_=b_qkv[2 * E : 3 * E].rearrange("(o n) -> o n", o=1),
        )
        tables = const.tile([P, 2, SEQ_GROUPS * TILES, TURNED], BF16)
        for which, table in enumerate((cos_tab, sin_tab)):
            nc.sync.dma_start(
                out=tables[:, which].rearrange("p (sg t) j -> p sg (t j)", sg=SEQ_GROUPS),
                in_=table.rearrange("(sg p t) j -> p sg (t j)", sg=SEQ_GROUPS, p=P, t=TILES),
            )
        w_raw = const.tile([P, 2 * 3 * E], U8, align_bytes=64)
        nc.sync.dma_start(
            out=w_raw[:].bitcast(I32),
            in_=W_qkv_words.rearrange("o p n -> (o p) n").bitcast(I32),
        )
        ones = const.tile([P, P], BF16)
        nc.vector.memset(ones[:], 1.0)
        for g in range(1, GROUPS):
            load_x(g)

        ident = const.tile([P, P], F32)
        make_identity(nc, ident[:])
        ident_bf = const.tile([P, P], BF16)
        make_identity(nc, ident_bf[:])
        swap = const.tile([P, P], F32)
        ident_halves = ident[:].rearrange("p (a b c) -> p a b c", b=2, c=HALF)
        swap_halves = swap[:].rearrange("p (a b c) -> p a b c", b=2, c=HALF)
        for b in range(2):
            nc.vector.tensor_copy(out=swap_halves[:, :, b, :], in_=ident_halves[:, :, 1 - b, :])

        cos, sin = tables[:, 0], tables[:, 1]
        lo, hi = slice(0, HALF), slice(HALF, TURNED)
        factor_rows = const.tile([P, SEQ_GROUPS * TILES, 2, BLOCK_HEADS, TURNED], BF16)

        def make_factor_rows(engine, sg):
            tiles = slice(sg * TILES, (sg + 1) * TILES)
            for o, cols, table, sign in ((0, slice(0, TURNED), cos[:, tiles, :], 1.0),
                                         (1, lo, sin[:, tiles, hi], 1.0), (1, hi, sin[:, tiles, lo], -1.0)):
                width = cols.stop - cols.start
                engine.tensor_scalar(
                    out=factor_rows[:, tiles, o, :, cols],
                    in0=table.unsqueeze(2).to_broadcast([P, TILES, BLOCK_HEADS, width]),
                    scalar1=sign, scalar2=0.0, op0=ALU.mult, op1=ALU.add,
                )

        factors = const.tile([P, SEQ_GROUPS, 2, GROUP], BF16)

        def turn_factors(sg):
            bank = psum_r.tile([P, 2, TILES, P], BF16, tag="r")
            for o in range(2):
                for t in range(TILES):
                    nc.tensor.transpose(
                        out=bank[:, o, t, :],
                        in_=factor_rows[:, sg * TILES + t, o].rearrange("p h i -> p (h i)"),
                        identity=ident_bf[:],
                    )
            nc.scalar.copy(out=factors[:, sg].rearrange("p o c -> p (o c)"), in_=bank[:].rearrange("p o t c -> p (o t c)"))

        w_qk = const.tile([P, 2 * 2 * E], U8, align_bytes=64)
        ws_qk = const.tile([P, 2 * E], U8, align_bytes=64)

        def sort_weight_words():
            nc.vector.tensor_copy(
                out=w_qk[:].bitcast(I32).rearrange("p (c h b) -> p c h b", c=2, h=QK_HEADS),
                in_=w_raw[:, 0 : 2 * 2 * E].bitcast(I32).rearrange("p (h c b) -> p c h b", h=QK_HEADS, c=2),
            )

        def sort_weight_scales():
            nc.vector.tensor_copy(
                out=ws_qk[:].bitcast(I32).rearrange("p (c h b) -> p c h b", c=2, h=QK_HEADS),
                in_=ws_raw[:, 0 : 2 * E].bitcast(I32).rearrange("p (h c b) -> p c h b", h=QK_HEADS, c=2),
            )

        def weight_columns(kind, first, count):
            words, plane, base = {
                "turned": (w_qk, ws_qk, 0),
                "plain": (w_qk, ws_qk, E),
                "v": (w_raw, ws_raw, 2 * E),
            }[kind]
            start = base + first
            return words[:, 2 * start : 2 * (start + count)].bitcast(FP4X4), plane[:, start : start + count]

        sorted_words = {}

        def sort_x_words(g, pair):
            x_words = x_tiles[g][:].bitcast(F32)
            sorted_words[g, pair] = stage.tile([P, 2, 2, P], F32, name="sorted_words")
            nc.scalar.copy(
                out=sorted_words[g, pair][:],
                in_=x_words[:, pair * E : (pair + 1) * E].rearrange("p (i c u) -> p i u c", i=2, u=2),
            )

        def transpose_x(g, pair, grouped):
            x_words = x_tiles[g][:].bitcast(F32)
            xt = psum_px.tile([P, 2, 2, P], F32, tag="px")
            for i in range(2):
                first = (2 * pair + i) * (E // 2)
                for u in range(2):
                    if (g, pair) in sorted_words:
                        words = sorted_words[g, pair][:, i, u, :]
                    else:
                        words = x_words[:, first + u : first + E // 2 : 2]
                    nc.tensor.transpose(out=xt[:, i, u, :], in_=words, identity=ident[:])
            grouped_words = grouped[:].bitcast(F32).rearrange("p (c u) -> p c u", u=2)
            nc.scalar.copy(
                out=grouped_words[:, 2 * P * pair : 2 * P * (pair + 1), :].rearrange(
                    "p (i c) u -> p i c u", i=2
                ),
                in_=xt[:].rearrange("p i u c -> p i c u"),
            )

        def quantise(grouped):
            codes = stage.tile([P, GROUP], U32, align_bytes=64)
            scales = stage.tile([P, GROUP], U8, align_bytes=64)
            nc.vector.quantize_mx(out=codes[:].bitcast(FP8X4), scales=scales[:], in_=grouped[:])
            return codes, scales

        def turned_block(xq, g, k, products):
            codes, scales = xq
            w_words, w_plane = weight_columns("turned", k * P, P)
            acc = psum_feat.tile([P, GROUP], F32)
            nc.tensor.matmul_mx(
                out=acc[:],
                lhsT=w_words,
                lhsT_scale=w_plane,
                rhs=codes[:].bitcast(FP8X4),
                rhs_scale=scales[:],
                start=True,
                stop=True,
            )
            nc.vector.scalar_tensor_tensor(
                out=products[:, k],
                in0=acc[:].unsqueeze(1).to_broadcast([P, 2, GROUP]),
                scalar=bias_col[:, k : k + 1],
                in1=factors[:, g % SEQ_GROUPS],
                op0=ALU.add,
                op1=ALU.mult,
            )

        def token_major(xq, kind, t, pool, tag):
            codes, scales = xq
            w_words, w_plane = weight_columns(kind, 0, E)
            bank = pool.tile([P, E], F32, tag=tag)
            nc.tensor.matmul_mx(
                out=bank[:],
                lhsT=codes[:, t * P : (t + 1) * P].bitcast(FP8X4),
                lhsT_scale=scales[:, t * P : (t + 1) * P],
                rhs=w_words,
                rhs_scale=w_plane,
                start=True,
                stop=True,
            )
            return bank

        def plain_features(xq, t, qk_out):
            plain = token_major(xq, "plain", t, psum_px, "px")
            nc.vector.tensor_tensor(
                out=qk_out[:, :, t, :, TURNED:HEAD_DIM],
                in0=plain[:].rearrange("p (q h j) -> p q h j", q=2, h=HEADS),
                in1=free_bias[:, 0, :].rearrange("p (q h j) -> p q h j", q=2, h=HEADS),
                op=ALU.add,
            )

        def v_features(xq, t, v_raw):
            v_bank = token_major(xq, "v", t, psum_v, "v")
            nc.scalar.copy(out=v_raw[:, t, :], in_=v_bank[:])

        def finish_v(g, pair, v_raw, v_out):
            tiles = slice(2 * pair, 2 * pair + 2)
            nc.gpsimd.tensor_tensor(
                out=v_out[:, tiles, :],
                in0=v_raw[:, tiles, :],
                in1=free_bias[:, 1, :].unsqueeze(1).to_broadcast([P, 2, E]),
                op=ALU.add,
            )

        def store_v(g, pair, v_out):
            nc.sync.dma_start(
                out=v_groups[g][:, 2 * pair * E : (2 * pair + 2) * E],
                in_=v_out[:, 2 * pair : 2 * pair + 2, :].rearrange("p t n -> p (t n)"),
            )

        def finish_turned(t, products, qk_out):
            r = psum_r.tile([P, E], F32)
            for o, moving in enumerate((ident, swap)):
                for k in range(BLOCKS):
                    nc.tensor.matmul(
                        out=r[:, k * P : (k + 1) * P],
                        lhsT=products[:, k, o, t * P : (t + 1) * P],
                        rhs=moving[:],
                        is_transpose=True,
                        start=(o == 0 and k == 0),
                        stop=(o == 1 and k == BLOCKS - 1),
                    )
            nc.scalar.copy(
                out=qk_out[:, :, t, :, 0:TURNED],
                in_=r[:].rearrange("p (q h j) -> p q h j", q=2, h=HEADS),
            )

        def store_qk(g, first, count, qk_out):
            for q, dram in enumerate((q_groups, k_groups)):
                nc.sync.dma_start(
                    out=dram[g][:, first * E : (first + count) * E],
                    in_=qk_out[:, q, first : first + count].rearrange("p t h d -> p (t h d)"),
                )

        grouped = {0: stage.tile([P, GROUP * PACK], BF16, align_bytes=64, name="grouped")}
        for pair in range(PAIRS):
            transpose_x(0, pair, grouped[0])
        bias_blocks_f32 = const.tile([P, P], F32)
        nc.vector.tensor_copy(out=bias_blocks_f32[:], in_=bias_blocks[:])
        free_bias = const.tile([P, 2, E], F32)
        for which in range(2):
            bias_bank = psum_v.tile([P, E], F32, tag="v")
            nc.tensor.matmul(out=bias_bank[:], lhsT=ones[:], rhs=bias_rows[:, which, :], start=True, stop=True)
            nc.scalar.copy(out=free_bias[:, which, :], in_=bias_bank[:])
        bias_t = psum_r.tile([P, P], F32, tag="r")
        nc.tensor.transpose(out=bias_t[:], in_=bias_blocks_f32[:], identity=ident[:])
        make_factor_rows(nc.vector, 0)
        for sg in range(1, SEQ_GROUPS):
            make_factor_rows(nc.gpsimd, sg)
        turn_factors(0)
        sort_weight_scales()
        sort_weight_words()
        xq = {0: quantise(grouped[0])}
        bias_col = const.tile([P, BLOCKS], F32)
        nc.vector.tensor_copy(out=bias_col[:], in_=bias_t[:, 0:BLOCKS])
        grouped[1] = stage.tile([P, GROUP * PACK], BF16, align_bytes=64, name="grouped")
        transpose_x(1, 0, grouped[1])
        sort_x_words(1, 1)

        products, qk_outs, v_raws, v_outs = {}, {}, {}, {}
        for i in range(GROUPS + 1):
            if i < GROUPS:
                products[i] = stage.tile([P, BLOCKS, 2, GROUP], F32, name="products")
                qk_outs[i] = outs.tile([P, 2, TILES, HEADS, HEAD_DIM], F32, name="qk_out")
                v_raws[i] = stage.tile([P, TILES, E], F32, name="v_raw")
                v_outs[i] = outs.tile([P, TILES, E], F32, name="v_out")
            for half in range(PAIRS):
                a, b = 2 * half, 2 * half + 1
                if i < GROUPS:
                    plain_features(xq[i], a, qk_outs[i])
                    turned_block(xq[i], i, a, products[i])
                    v_features(xq[i], a, v_raws[i])
                    v_features(xq[i], b, v_raws[i])
                    if half == 1 and i + 1 < GROUPS:
                        xq[i + 1] = quantise(grouped[i + 1])
                    plain_features(xq[i], b, qk_outs[i])
                    turned_block(xq[i], i, b, products[i])
                    finish_v(i, half, v_raws[i], v_outs[i])
                if i + 2 < GROUPS:
                    sort_x_words(i + 2, half)
                if half == 0 and i + 1 < GROUPS:
                    transpose_x(i + 1, 1, grouped[i + 1])
                if half == 1 and i + 2 < GROUPS:
                    grouped[i + 2] = stage.tile([P, GROUP * PACK], BF16, align_bytes=64, name="grouped")
                    transpose_x(i + 2, 0, grouped[i + 2])
                if i >= 1:
                    finish_turned(a, products[i - 1], qk_outs[i - 1])
                    if i == GROUPS:
                        store_qk(i - 1, a, 1, qk_outs[i - 1])
                    finish_turned(b, products[i - 1], qk_outs[i - 1])
                    if i == GROUPS:
                        store_qk(i - 1, b, 1, qk_outs[i - 1])
                    else:
                        store_qk(i - 1, a, 2, qk_outs[i - 1])
                if i < GROUPS:
                    store_v(i, half, v_outs[i])
                if i == 0:
                    for sg in ((1,), (2, 3))[half]:
                        turn_factors(sg)
